import numpy as np
import ml_dtypes


def mxq(x, axis, fmt="e4m3"):
    dtype, down = {"e4m3": (ml_dtypes.float8_e4m3fn, 7), "e5m2": (ml_dtypes.float8_e5m2, 14)}[fmt]
    v = np.moveaxis(np.asarray(x, np.float32).astype(ml_dtypes.bfloat16).astype(np.float64), axis, -1)
    blocks = v.reshape(v.shape[:-1] + (-1, 32))
    amax = np.abs(blocks).max(-1, keepdims=True)
    byte = np.maximum(np.where(amax > 0, np.frexp(amax)[1] - 1 + 127, 0) - down, 1)
    scale = np.exp2(byte - 127.0)
    codes = (blocks / scale).astype(np.float32).astype(dtype).astype(np.float64)
    return np.moveaxis((codes * scale).reshape(v.shape), -1, axis)


WIDE = False


def mx_kscale(k):
    if not WIDE:
        return np.ones(k)
    levels = np.array([10, -10, 5, -5, 0])
    if k % 512:
        return np.exp2(np.random.permutation(np.resize(levels, k // 32))).repeat(32)
    a = np.empty((k // 512, 16))
    for p in range(k // 512):
        a[p, :8] = np.random.permutation(np.resize(levels, 8))
        for g in range(8):
            far = levels[np.abs(levels - a[p, g]) >= 10]
            a[p, g + 8] = far[np.random.randint(len(far))]
    return np.exp2(a.ravel()).repeat(32)


BF16 = ml_dtypes.bfloat16


def bf(x):
    return np.asarray(x, np.float32).astype(BF16)


def f64(x):
    return np.asarray(x).astype(np.float64)


B, I, J, K, D = 1024, 1024, 256, 4, 2
EPS = 1e-8


def caps_sum(xf, ws):
    return (xf.transpose(2, 0, 1) @ ws.transpose(2, 1, 0)).transpose(1, 2, 0)


def setup_inputs():
    t = mx_kscale(B)
    u = mx_kscale(I)
    c = 2.0 / np.sqrt(J * D * (K * K / 4.0 + K / 12.0))
    x0 = bf(np.random.standard_normal((B, J, D)))
    w0 = bf(np.random.random((I, J, K, D)) * c)
    g = bf(np.random.standard_normal((B, I, D)) * np.exp2(np.random.randint(-6, 1, (B, 1, 1))) * 8.0
           / t[:, None, None] * u[None, :, None])
    s = caps_sum(f64(x0), f64(w0).sum(axis=2))
    return {"X": bf(f64(x0) * t[:, None, None]),
            "weight": bf(f64(w0) / u[:, None, None, None]),
            "s": np.asarray(s, np.float32), "grad_out": g}


def reference(X, weight, s, grad_out):
    sf = f64(s)
    g = f64(grad_out)
    n2 = np.sum(sf * sf, axis=-1, keepdims=True)
    n = np.sqrt(n2)
    f = n2 / (1.0 + n2) / (n + EPS)
    c = 2.0 / ((1.0 + n2) ** 2 * (n + EPS)) - n / ((1.0 + n2) * (n + EPS) ** 2)
    p = np.sum(g * sf, axis=-1, keepdims=True)
    ds = f * g + c * p * sf
    ws = f64(weight).sum(axis=2)
    di = mxq(ds, 1, "e5m2")
    wq = mxq(ws, 0, "e4m3")
    gx = di.transpose(2, 0, 1) @ wq.transpose(2, 0, 1)
    db = mxq(ds, 0, "e5m2")
    xq = mxq(f64(X), 0, "e4m3")
    dws = db.transpose(2, 1, 0) @ xq.transpose(2, 0, 1)
    dws = dws.transpose(1, 2, 0)
    gw = np.repeat(dws[:, :, None, :], K, axis=2)
    return gx.transpose(1, 2, 0), gw

@@ -1,0 +1,472 @@
+from contextlib import ExitStack
+
+import concourse.masks as masks
+import concourse.mybir as mybir
+
+F32 = mybir.dt.float32
+BF16 = mybir.dt.bfloat16
+U32 = mybir.dt.uint32
+U8 = mybir.dt.uint8
+I32 = mybir.dt.int32
+E4 = mybir.dt.float8_e4m3fn_x4
+E5 = mybir.dt.float8_e5m2_x4
+ALU = mybir.AluOpType
+ACT = mybir.ActivationFunctionType
+AX = mybir.AxisListType
+
+P = 128
+EPS = 1e-8
+TINY = 1e-30
+FLOPS = 2 * 2 * 2 * 1024 * 1024 * 256
+NU = 16
+BUD_SA = 1.0
+BUD_SB = 1.9
+BUD_VA = 0.0
+BUD_VB = 1.6
+BUD_PE = 2.0
+W1_ON_S = True
+PE_LAG = 1
+
+
+def tile_primary_capsule_t_v_kernel(tc, X, weight, s, grad_out, out_0, out_1):
+    nc = tc.nc
+    xv = X.rearrange("(g p t) j d -> p g (t j d)", g=2, p=P, t=4)
+    wv = weight.rearrange("(h p t) j k d -> p h t (j k d)", h=2, p=P, t=4)
+    sv = s.rearrange("(g p t) (q i) d -> p g t q (i d)", g=2, p=P, t=4, q=4)
+    gv = grad_out.rearrange("(g p t) (q i) d -> p g t q (i d)", g=2, p=P, t=4, q=4)
+    o0v = out_0.rearrange("(g p t) j d -> p g t (j d)", g=2, p=P, t=4)
+    o1v = out_1.rearrange("(m p) j k d -> p m (j k d)", p=P)
+
+    with ExitStack() as ctx:
+        ctx.enter_context(tc.manual_schedule())
+        const = ctx.enter_context(tc.tile_pool(name="const", bufs=1))
+        keep = ctx.enter_context(tc.tile_pool(name="keep", bufs=1))
+        ld = ctx.enter_context(tc.tile_pool(name="ld", bufs=3))
+        wide = ctx.enter_context(tc.tile_pool(name="wide", bufs=2))
+        nar = ctx.enter_context(tc.tile_pool(name="nar", bufs=2))
+        stg = ctx.enter_context(tc.tile_pool(name="stg", bufs=2))
+        ps_n = ctx.enter_context(tc.psum_pool(name="ps_n", bufs=2))
+        ps_r = ctx.enter_context(tc.psum_pool(name="ps_r", bufs=1))
+        ps_x = ctx.enter_context(tc.psum_pool(name="ps_x", bufs=2))
+        ps_a = ctx.enter_context(tc.psum_pool(name="ps_a", bufs=2))
+
+        ident = const.tile([P, P], F32, name="ident")
+        masks.make_identity(nc, ident[:])
+        tiny = const.tile([P, 1], F32, name="tiny")
+        nc.vector.memset(tiny[:], TINY)
+        m2eps = const.tile([P, 1], F32, name="m2eps")
+        nc.vector.memset(m2eps[:], -2.0 * EPS)
+
+        mg = keep.tile([P, 2, 256, 2, 4], BF16, name="mg", align_bytes=64)
+        nc.vector.memset(mg[:].rearrange("p d j e t -> p (d j e t)").bitcast(I32), 0)
+        xc = keep.tile([P, 2048], U32, name="xc", align_bytes=64)
+        xs = keep.tile([P, 2048], U8, name="xs", align_bytes=64)
+        wc = keep.tile([P, 2048], U32, name="wc", align_bytes=64)
+        ws = keep.tile([P, 2048], U8, name="ws", align_bytes=64)
+        c2 = {}
+        s2 = {}
+        for h in range(2):
+            c2[h] = keep.tile([P, 2048], U32, name="c2_%d" % h, align_bytes=64)
+            s2[h] = keep.tile([P, 2048], U8, name="s2_%d" % h, align_bytes=64)
+
+        T = {}
+        bg = {"C": [], "V": [], "W": [], "PE": []}
+        now = [0]
+
+        def later(eng, cost, fn, delay=1, first=False):
+            if first:
+                bg[eng].insert(0, (now[0] + delay, cost, fn))
+            else:
+                bg[eng].append((now[0] + delay, cost, fn))
+
+        def run_bg(eng, budget, spent=0.0):
+            k = 0
+            while k < len(bg[eng]) and spent < budget:
+                if bg[eng][k][0] <= now[0]:
+                    piece = bg[eng].pop(k)
+                    spent += piece[1]
+                    piece[2]()
+                else:
+                    k += 1
+            return spent
+
+        side = ["S"]
+
+        def cp(out, in_):
+            if side[0] == "S":
+                nc.scalar.copy(out=out, in_=in_)
+            else:
+                nc.vector.tensor_copy(out=out, in_=in_)
+
+        def load_chunk(c):
+            q, g = c // 2, c % 2
+            T["s", c] = ld.tile([P, 4, 512], F32, name="s_sb")
+            T["g", c] = ld.tile([P, 4, 512], BF16, name="g_sb")
+            step = 2 if c == 0 else 4
+            for t in range(0, 4, step):
+                nc.sync.dma_start(out=T["s", c][:, t : t + step], in_=sv[:, g, t : t + step, q, :])
+                nc.sync.dma_start(out=T["g", c][:, t : t + step], in_=gv[:, g, t : t + step, q, :])
+
+        def quant_m(codes, scales, o):
+            nc.vector.quantize_mx(
+                out=codes[:, o : o + 1024].bitcast(E4),
+                scales=scales[:, o : o + 1024],
+                in_=mg[:].rearrange("p d j e t -> p (d j e t)"),
+            )
+
+        def x_load(g):
+            T["x", g] = ld.tile([P, 4096], BF16, name="xw_sb", bufs=2)
+            nc.sync.dma_start(out=T["x", g][:, 0:2048], in_=xv[:, g, :])
+
+        def x_copy(g, d):
+            cp(
+                out=mg[:, d, :, d, :],
+                in_=T["x", g][:, 0:2048].rearrange("p (t j d) -> p d j t", t=4, j=256, d=2)[:, d],
+            )
+            if d == 1:
+                later("V", 0.95, lambda: x_quant(g))
+                w_load(0, g)
+
+        def x_quant(g):
+            quant_m(xc, xs, g * 1024)
+            if g == 0:
+                for e in range(2):
+                    later("C", 0.95, lambda e=e: x_copy(1, e))
+            else:
+                for h in range(2):
+                    for jh in range(2):
+                        for e in range(2):
+                            later("W", 1.75, lambda h=h, jh=jh, e=e: w_sum(h, jh, e))
+                    later("W", 0.95, lambda h=h: quant_m(wc, ws, h * 1024))
+
+        def w_load(h, jh):
+            T["w", h, jh] = ld.tile([P, 4096], BF16, name="xw_sb", bufs=2)
+            nc.sync.dma_start(
+                out=T["w", h, jh][:].rearrange("p (t w) -> p t w", t=4), in_=wv[:, h, :, jh * 1024 : (jh + 1) * 1024]
+            )
+
+        def w_sum(h, jh, d):
+            with nc.allow_low_precision(reason="the engine sums in float32 and rounds once to bfloat16"):
+                nc.vector.tensor_reduce(
+                    out=mg[:, d, jh * 128 : (jh + 1) * 128, d, :],
+                    in_=T["w", h, jh][:].rearrange("p (t j k d) -> p d j t k", t=4, j=128, k=4, d=2)[:, d],
+                    axis=AX.X,
+                    op=ALU.add,
+                )
+            if d == 1 and h == 0:
+                w_load(1, jh)
+
+        def planes(u):
+            c, tp = u // 2, u % 2
+            s_pl = T["s", c][:, 2 * tp : 2 * tp + 2, :].rearrange("p t (i d) -> p t d i", d=2)
+            g_pl = T["g", c][:, 2 * tp : 2 * tp + 2, :].rearrange("p t (i d) -> p t d i", d=2)
+            return s_pl, g_pl
+
+        def st_sq(u):
+            T["sq", u] = wide.tile([P, 2, 2, 256], F32, name="sq")
+            nc.scalar.activation(out=T["sq", u][:], in_=planes(u)[0], func=ACT.Square)
+
+        def st_gs(u):
+            s_pl, g_pl = planes(u)
+            T["gs", u] = wide.tile([P, 2, 2, 256], F32, name="gs")
+            nc.gpsimd.tensor_tensor(out=T["gs", u][:], in0=g_pl, in1=s_pl, op=ALU.mult)
+
+        def add_over_d(src, dst):
+            for tl in range(2):
+                for ib in range(2):
+                    b = (tl * 2 + ib) * 128
+                    for d in range(2):
+                        nc.tensor.matmul(
+                            out=dst[:, b : b + 128],
+                            lhsT=src[:, tl, d, ib * 128 : (ib + 1) * 128],
+                            rhs=ident[:],
+                            is_transpose=True,
+                            start=(d == 0),
+                            stop=(d == 1),
+                        )
+
+        def st_n2T(u):
+            T["n2T", u] = ps_n.tile([P, 512], F32, name="n2T")
+            add_over_d(T["sq", u], T["n2T", u])
+
+        def st_pT(u):
+            T["pT", u] = ps_r.tile([P, 512], F32, name="fp")
+            add_over_d(T["gs", u], T["pT", u])
+
+        def nt(name, u):
+            T[name, u] = nar.tile([P, 512], F32, name=name)
+            return T[name, u]
+
+        def st_rho(u):
+            nc.scalar.activation(out=nt("rho", u)[:], in_=T["n2T", u][:], func=ACT.Abs_reciprocal_sqrt, bias=tiny[:])
+
+        def st_n(u):
+            nc.vector.tensor_tensor(out=nt("n_t", u)[:], in0=T["n2T", u][:], in1=T["rho", u][:], op=ALU.mult)
+
+        def st_w0(u):
+            nc.vector.scalar_tensor_tensor(
+                out=nt("w_t", u)[:], in0=T["n2T", u][:], scalar=1.0, in1=T["n_t", u][:], op0=ALU.subtract, op1=ALU.mult
+            )
+
+        def st_x(u):
+            nc.gpsimd.tensor_scalar(out=nt("x_t", u)[:], in0=T["n_t", u][:], scalar1=1.0, scalar2=EPS, op0=ALU.mult, op1=ALU.add)
+
+        def st_w1(u):
+            if W1_ON_S:
+                nc.scalar.activation(out=T["w_t", u][:], in_=T["w_t", u][:], func=ACT.Identity, bias=m2eps[:])
+            else:
+                nc.gpsimd.tensor_scalar(
+                    out=T["w_t", u][:], in0=T["w_t", u][:], scalar1=1.0, scalar2=-2.0 * EPS, op0=ALU.mult, op1=ALU.add
+                )
+
+        def st_D(u):
+            nc.vector.scalar_tensor_tensor(
+                out=nt("d_t", u)[:], in0=T["n2T", u][:], scalar=1.0, in1=T["x_t", u][:], op0=ALU.add, op1=ALU.mult
+            )
+
+        def st_pw(u):
+            nc.vector.tensor_tensor(out=nt("pw", u)[:], in0=T["pT", u][:], in1=T["w_t", u][:], op=ALU.mult)
+
+        def st_R(u):
+            nc.scalar.activation(out=nt("r_t", u)[:], in_=T["d_t", u][:], func=ACT.Abs_reciprocal_sqrt)
+            st_w1(u)
+            nc.scalar.activation(out=T["r_t", u][:], in_=T["r_t", u][:], func=ACT.Square)
+            nc.scalar.activation(out=nt("r2", u)[:], in_=T["r_t", u][:], func=ACT.Square)
+
+        def st_fT(u):
+            nc.vector.tensor_tensor(out=nt("fT", u)[:], in0=T["n2T", u][:], in1=T["r_t", u][:], op=ALU.mult)
+
+        def st_eT(u):
+            nc.gpsimd.tensor_tensor(out=T["pw", u][:], in0=T["pw", u][:], in1=T["r2", u][:], op=ALU.mult)
+
+        def back(src, dst):
+            for b in range(0, 512, 128):
+                nc.tensor.transpose(out=dst[:, b : b + 128], in_=src[:, b : b + 128], identity=ident[:])
+
+        def st_fN(u):
+            T["fN", u] = ps_r.tile([P, 512], F32, name="fp")
+            back(T["fT", u], T["fN", u])
+
+        def st_eN(u):
+            T["eN", u] = ps_r.tile([P, 512], F32, name="eN")
+            back(T["pw", u], T["eN", u])
+
+        def over_d(t):
+            return t[:].rearrange("p (t i) -> p t i", t=2).unsqueeze(2).to_broadcast([P, 2, 2, 256])
+
+        def st_fg(u):
+            T["fg", u] = wide.tile([P, 2, 2, 256], F32, name="fg")
+            nc.vector.tensor_tensor(out=T["fg", u][:], in0=over_d(T["fN", u]), in1=planes(u)[1], op=ALU.mult)
+
+        def st_es(u):
+            T["es", u] = wide.tile([P, 2, 2, 256], F32, name="es")
+            nc.vector.tensor_tensor(out=T["es", u][:], in0=over_d(T["eN", u]), in1=planes(u)[0], op=ALU.mult)
+
+        def st_sub(u):
+            c, tp = u // 2, u % 2
+            q, g = c // 2, c % 2
+            h, qq = q // 2, q % 2
+            if qq == 0 and tp == 0:
+                T["a", h, g] = stg.tile([P, 4, 2, 512], BF16, name="a_t", align_bytes=64)
+            nc.gpsimd.tensor_tensor(
+                out=T["a", h, g][:, 2 * tp : 2 * tp + 2, :, qq * 256 : (qq + 1) * 256],
+                in0=T["fg", u][:],
+                in1=T["es", u][:],
+                op=ALU.subtract,
+            )
+            if qq == 1:
+                T["g2", u] = stg.tile([P, 2, 1024], BF16, name="g2", align_bytes=64)
+                for tl in range(2):
+                    later("PE", 0.45, lambda tl=tl: turn(u, tl))
+            if tp == 1:
+                T["bt", c] = stg.tile([P, 2, 256, 4], BF16, name="bt", align_bytes=64)
+                for d in (1, 0):
+                    later("C", 0.9, lambda d=d: weave(c, d), 1, True)
+
+        def weave(c, d):
+            q, g = c // 2, c % 2
+            h, qq = q // 2, q % 2
+            cp(out=T["bt", c][:, d], in_=T["a", h, g][:, :, d, qq * 256 : (qq + 1) * 256].rearrange("p t i -> p i t"))
+            if d == 1:
+                later("V", 0.5, lambda: quant_b(c))
+
+        def quant_b(c):
+            q, g = c // 2, c % 2
+            T["c1", c] = stg.tile([P, 512], U32, name="c1", bufs=4, align_bytes=64)
+            T["s1", c] = stg.tile([P, 512], U8, name="s1", bufs=4, align_bytes=64)
+            nc.vector.quantize_mx(
+                out=T["c1", c][:].bitcast(E5), scales=T["s1", c][:], in_=T["bt", c][:].rearrange("p d i t -> p (d i t)")
+            )
+            if g == 1:
+                later("PE", 0.9, lambda: mm_out1(q, 0))
+                if q == 3:
+                    later("PE", 0.9, lambda: mm_out1(q, 1))
+
+        spare = [(ps_a, "acc"), (ps_a, "acc"), (ps_r, "fp"), (ps_r, "eN"), (ps_n, "n2T"), (ps_n, "n2T")]
+        n_acc = [0]
+
+        def new_acc():
+            if not drain[0]:
+                return ps_a.tile([P, 512], F32, name="acc")
+            n_acc[0] += 1
+            pool, name = spare[n_acc[0] % len(spare)]
+            return pool.tile([P, 512], F32, name=name)
+
+        def mm_out1(q, ib):
+            acc = new_acc()
+            for g in range(2):
+                for d in range(2):
+                    ox = (g * 2 + d) * 512
+                    oc = d * 256 + ib * 128
+                    nc.tensor.matmul_mx(
+                        out=acc[:],
+                        lhsT=T["c1", q * 2 + g][:, oc : oc + 128].bitcast(E5),
+                        lhsT_scale=T["s1", q * 2 + g][:, oc : oc + 128],
+                        rhs=xc[:, ox : ox + 512].bitcast(E4),
+                        rhs_scale=xs[:, ox : ox + 512],
+                        start=(g == 0 and d == 0),
+                        stop=(g == 1 and d == 1),
+                    )
+            o1 = stg.tile([P, 256, 4, 2], F32, name="o1")
+            for jh in range(2):
+                later("C", 0.9, lambda jh=jh: out1_copy(q, ib, acc, o1, jh), PE_LAG)
+
+        def out1_copy(q, ib, acc, o1, jh):
+            cp(
+                out=o1[:, jh * 128 : (jh + 1) * 128],
+                in_=acc[:, jh * 256 : (jh + 1) * 256].rearrange("p (j d) -> p j d", d=2).unsqueeze(2).to_broadcast([P, 128, 4, 2]),
+            )
+            if q == 3:
+                nc.sync.dma_start(
+                    out=o1v[:, q * 2 + ib, jh * 1024 : (jh + 1) * 1024],
+                    in_=o1[:, jh * 128 : (jh + 1) * 128].rearrange("p j k d -> p (j k d)"),
+                )
+            elif jh == 1:
+                nc.sync.dma_start(out=o1v[:, q * 2 + ib, :], in_=o1[:].rearrange("p j k d -> p (j k d)"))
+                if ib == 0:
+                    later("PE", 0.9, lambda: mm_out1(q, 1), 0)
+
+        def turn(u, tl):
+            c, tp = u // 2, u % 2
+            q, g = c // 2, c % 2
+            xt = ps_x.tile([P, 512], F32, name="xt")
+            for d in range(2):
+                aw = T["a", q // 2, g][:, 2 * tp + tl, d, :].bitcast(F32)
+                for w in range(2):
+                    b = (d * 2 + w) * 128
+                    nc.tensor.transpose(out=xt[:, b : b + 128], in_=aw[:, w:256:2], identity=ident[:])
+            later("C", 0.45, lambda: turn_copy(u, tl, xt), PE_LAG)
+
+        def turn_copy(u, tl, xt):
+            cp(
+                out=T["g2", u][:, tl].bitcast(F32).rearrange("p (d r w) -> p d r w", d=2, r=128, w=2),
+                in_=xt[:].rearrange("p (d w r) -> p d r w", d=2, w=2, r=128),
+            )
+            if tl == 1:
+                later("V", 0.55, lambda: quant_i(u))
+
+        def quant_i(u):
+            c, tp = u // 2, u % 2
+            q, g = c // 2, c % 2
+            h = q // 2
+            o = (g * 4 + 2 * tp) * 256
+            nc.vector.quantize_mx(
+                out=c2[h][:, o : o + 512].bitcast(E5), scales=s2[h][:, o : o + 512], in_=T["g2", u][:].rearrange("p t w -> p (t w)")
+            )
+            if h == 1:
+                for tl in range(2):
+                    later("PE", 0.9, lambda tl=tl: mm_out0(g, 2 * tp + tl), 1 + (0 if drain[0] else 2 * tl))
+
+        def mm_out0(g, t):
+            acc = new_acc()
+            o = (g * 4 + t) * 256
+            for hh in range(2):
+                for d in range(2):
+                    ow = (hh * 2 + d) * 512
+                    nc.tensor.matmul_mx(
+                        out=acc[:],
+                        lhsT=c2[hh][:, o + d * 128 : o + (d + 1) * 128].bitcast(E5),
+                        lhsT_scale=s2[hh][:, o + d * 128 : o + (d + 1) * 128],
+                        rhs=wc[:, ow : ow + 512].bitcast(E4),
+                        rhs_scale=ws[:, ow : ow + 512],
+                        start=(hh == 0 and d == 0),
+                        stop=(hh == 1 and d == 1),
+                    )
+            later("C", 0.45, lambda: out0_copy(g, t, acc), PE_LAG)
+
+        def out0_copy(g, t, acc):
+            o0 = stg.tile([P, 512], F32, name="o0", bufs=3)
+            cp(out=o0[:], in_=acc[:])
+            nc.sync.dma_start(out=o0v[:, g, t, :], in_=o0[:])
+
+        def ok(u):
+            return 0 <= u < NU
+
+        def left():
+            return len(bg["C"]) + len(bg["V"]) + len(bg["W"]) + len(bg["PE"])
+
+        drain = [False]
+
+        def slot(bud_c, bud_v, bud_pe):
+            if drain[0]:
+                while len(bg["C"]) > 0 and run_bg("C", 0.1) > 0.0:
+                    side[0] = "V" if side[0] == "S" else "S"
+                side[0] = "S"
+                run_bg("W", 9.0, run_bg("V", 9.0))
+                run_bg("PE", 9.0)
+            else:
+                run_bg("C", bud_c)
+                run_bg("W", bud_v, run_bg("V", bud_v))
+                run_bg("PE", bud_pe)
+
+        load_chunk(0)
+        load_chunk(1)
+        x_load(0)
+        x_load(1)
+        load_chunk(2)
+        for d in range(2):
+            later("C", 0.95, lambda d=d: x_copy(0, d), 3)
+        st_sq(0)
+        st_gs(0)
+        st_n2T(0)
+        it = 0
+        while it < NU + 2 or left() > 0:
+            u = it
+            drain[0] = it >= NU
+            now[0] = 2 * it
+            if ok(u):
+                st_rho(u)
+                st_n(u)
+                st_x(u)
+            if ok(u + 1):
+                st_sq(u + 1)
+            if ok(u - 1):
+                st_fg(u - 1)
+            if ok(u):
+                st_pT(u)
+            if ok(u + 1):
+                st_n2T(u + 1)
+            if ok(u):
+                st_D(u)
+                st_w0(u)
+            if ok(u - 2):
+                st_sub(u - 2)
+            slot(BUD_SA, BUD_VA, BUD_PE)
+            if ok(u):
+                st_R(u)
+            if ok(u - 1):
+                st_es(u - 1)
+                if u % 2 == 0 and u // 2 + 2 < NU // 2:
+                    load_chunk(u // 2 + 2)
+            if ok(u):
+                st_pw(u)
+                st_fT(u)
+            if ok(u + 1):
+                st_gs(u + 1)
+            if ok(u):
+                st_eT(u)
+                st_fN(u)
+                st_eN(u)
+            now[0] = 2 * it + 1
+            slot(BUD_SB, BUD_VB, 0.0)
+            it += 1

@@ -19,13 +19,15 @@ EPS = 1e-8
 TINY = 1e-30
 FLOPS = 2 * 2 * 2 * 1024 * 1024 * 256
 NU = 16
-BUD_SA = 1.0
-BUD_SB = 1.9
-BUD_VA = 0.0
-BUD_VB = 1.6
+ORDER = ((0, 0), (0, 1), (1, 0), (1, 1), (2, 0), (2, 1), (3, 0), (3, 1))
+BUD_S = 2.6
+BUD_V = 1.6
 BUD_PE = 2.0
-W1_ON_S = True
-PE_LAG = 1
+XW_BUFS = 2
+W_LAG = 0
+V_SUBS = 2
+LATE = 14
+CUT = 15
 
 
 def tile_primary_capsule_t_v_kernel(tc, X, weight, s, grad_out, out_0, out_1):
@@ -38,7 +40,6 @@ def tile_primary_capsule_t_v_kernel(tc, X, weight, s, grad_out, out_0, out_1):
     o1v = out_1.rearrange("(m p) j k d -> p m (j k d)", p=P)
 
     with ExitStack() as ctx:
-        ctx.enter_context(tc.manual_schedule())
         const = ctx.enter_context(tc.tile_pool(name="const", bufs=1))
         keep = ctx.enter_context(tc.tile_pool(name="keep", bufs=1))
         ld = ctx.enter_context(tc.tile_pool(name="ld", bufs=3))
@@ -72,17 +73,23 @@ def tile_primary_capsule_t_v_kernel(tc, X, weight, s, grad_out, out_0, out_1):
         T = {}
         bg = {"C": [], "V": [], "W": [], "PE": []}
         now = [0]
+        drain = [False]
+        side = ["S"]
 
-        def later(eng, cost, fn, delay=1, first=False):
+        free = {"": 1, "x": 0, "w": 0, "xt": 2, "acc": 2}
+
+        def later(eng, cost, fn, delay=1, first=False, need=("",)):
+            if drain[0]:
+                delay = 0
             if first:
-                bg[eng].insert(0, (now[0] + delay, cost, fn))
+                bg[eng].insert(0, (now[0] + delay, cost, fn, need))
             else:
-                bg[eng].append((now[0] + delay, cost, fn))
+                bg[eng].append((now[0] + delay, cost, fn, need))
 
         def run_bg(eng, budget, spent=0.0):
             k = 0
             while k < len(bg[eng]) and spent < budget:
-                if bg[eng][k][0] <= now[0]:
+                if bg[eng][k][0] <= now[0] and all(free[r] > 0 for r in bg[eng][k][3]):
                     piece = bg[eng].pop(k)
                     spent += piece[1]
                     piece[2]()
@@ -90,22 +97,20 @@ def tile_primary_capsule_t_v_kernel(tc, X, weight, s, grad_out, out_0, out_1):
                     k += 1
             return spent
 
-        side = ["S"]
-
         def cp(out, in_):
             if side[0] == "S":
                 nc.scalar.copy(out=out, in_=in_)
             else:
                 nc.vector.tensor_copy(out=out, in_=in_)
 
-        def load_chunk(c):
-            q, g = c // 2, c % 2
-            T["s", c] = ld.tile([P, 4, 512], F32, name="s_sb")
-            T["g", c] = ld.tile([P, 4, 512], BF16, name="g_sb")
-            step = 2 if c == 0 else 4
-            for t in range(0, 4, step):
-                nc.sync.dma_start(out=T["s", c][:, t : t + step], in_=sv[:, g, t : t + step, q, :])
-                nc.sync.dma_start(out=T["g", c][:, t : t + step], in_=gv[:, g, t : t + step, q, :])
+        def load_chunk(c, parts):
+            q, g = ORDER[c]
+            if parts[0] == 0:
+                T["s", c] = ld.tile([P, 4, 512], F32, name="s_sb")
+                T["g", c] = ld.tile([P, 4, 512], BF16, name="g_sb")
+            a, b = parts
+            nc.sync.dma_start(out=T["s", c][:, a:b], in_=sv[:, g, a:b, q, :])
+            nc.sync.dma_start(out=T["g", c][:, a:b], in_=gv[:, g, a:b, q, :])
 
         def quant_m(codes, scales, o):
             nc.vector.quantize_mx(
@@ -115,8 +120,20 @@ def tile_primary_capsule_t_v_kernel(tc, X, weight, s, grad_out, out_0, out_1):
             )
 
         def x_load(g):
-            T["x", g] = ld.tile([P, 4096], BF16, name="xw_sb", bufs=2)
+            T["x", g] = ld.tile([P, 4096], BF16, name="xw_sb", bufs=XW_BUFS)
             nc.sync.dma_start(out=T["x", g][:, 0:2048], in_=xv[:, g, :])
+
+        def w_load(h, jh):
+            T["w", h, jh] = ld.tile([P, 4096], BF16, name="xw_sb", bufs=XW_BUFS)
+            nc.sync.dma_start(
+                out=T["w", h, jh][:].rearrange("p (t w) -> p t w", t=4), in_=wv[:, h, :, jh * 1024 : (jh + 1) * 1024]
+            )
+
+        loads = [lambda: w_load(0, 0), lambda: w_load(0, 1), lambda: x_load(0), lambda: x_load(1), lambda: w_load(1, 0), lambda: w_load(1, 1)]
+
+        def next_load():
+            if len(loads) > 0:
+                loads.pop(0)()
 
         def x_copy(g, d):
             cp(
@@ -124,26 +141,23 @@ def tile_primary_capsule_t_v_kernel(tc, X, weight, s, grad_out, out_0, out_1):
                 in_=T["x", g][:, 0:2048].rearrange("p (t j d) -> p d j t", t=4, j=256, d=2)[:, d],
             )
             if d == 1:
-                later("V", 0.95, lambda: x_quant(g))
-                w_load(0, g)
+                next_load()
+                later("V", 0.95, lambda: x_quant(g), 1, True)
 
         def x_quant(g):
             quant_m(xc, xs, g * 1024)
             if g == 0:
-                for e in range(2):
-                    later("C", 0.95, lambda e=e: x_copy(1, e))
+                for e in (1, 0):
+                    later("C", 0.95, lambda e=e: x_copy(1, e), 1, True)
             else:
-                for h in range(2):
-                    for jh in range(2):
-                        for e in range(2):
-                            later("W", 1.75, lambda h=h, jh=jh, e=e: w_sum(h, jh, e))
-                    later("W", 0.95, lambda h=h: quant_m(wc, ws, h * 1024))
+                free["x"] = 1
+                w_half(1)
 
-        def w_load(h, jh):
-            T["w", h, jh] = ld.tile([P, 4096], BF16, name="xw_sb", bufs=2)
-            nc.sync.dma_start(
-                out=T["w", h, jh][:].rearrange("p (t w) -> p t w", t=4), in_=wv[:, h, :, jh * 1024 : (jh + 1) * 1024]
-            )
+        def w_half(h):
+            for jh in range(2):
+                for e in range(2):
+                    later("W", 1.75, lambda jh=jh, e=e: w_sum(h, jh, e), W_LAG if jh == 0 else 1)
+            later("W", 0.95, lambda: w_quant(h))
 
         def w_sum(h, jh, d):
             with nc.allow_low_precision(reason="the engine sums in float32 and rounds once to bfloat16"):
@@ -153,8 +167,16 @@ def tile_primary_capsule_t_v_kernel(tc, X, weight, s, grad_out, out_0, out_1):
                     axis=AX.X,
                     op=ALU.add,
                 )
-            if d == 1 and h == 0:
-                w_load(1, jh)
+            if d == 1:
+                next_load()
+
+        def w_quant(h):
+            quant_m(wc, ws, h * 1024)
+            if h == 0:
+                for e in (1, 0):
+                    later("C", 0.95, lambda e=e: x_copy(0, e), 1, True)
+            else:
+                free["w"] = 1
 
         def planes(u):
             c, tp = u // 2, u % 2
@@ -163,7 +185,7 @@ def tile_primary_capsule_t_v_kernel(tc, X, weight, s, grad_out, out_0, out_1):
             return s_pl, g_pl
 
         def st_sq(u):
-            T["sq", u] = wide.tile([P, 2, 2, 256], F32, name="sq")
+            T["sq", u] = wide.tile([P, 2, 2, 256], F32, name="sq", bufs=1)
             nc.scalar.activation(out=T["sq", u][:], in_=planes(u)[0], func=ACT.Square)
 
         def st_gs(u):
@@ -193,51 +215,44 @@ def tile_primary_capsule_t_v_kernel(tc, X, weight, s, grad_out, out_0, out_1):
             T["pT", u] = ps_r.tile([P, 512], F32, name="fp")
             add_over_d(T["gs", u], T["pT", u])
 
-        def nt(name, u):
-            T[name, u] = nar.tile([P, 512], F32, name=name)
+        def nt(name, u, bufs=2):
+            T[name, u] = nar.tile([P, 512], F32, name=name, bufs=bufs)
             return T[name, u]
 
         def st_rho(u):
-            nc.scalar.activation(out=nt("rho", u)[:], in_=T["n2T", u][:], func=ACT.Abs_reciprocal_sqrt, bias=tiny[:])
+            nc.scalar.activation(out=nt("rho", u, 1)[:], in_=T["n2T", u][:], func=ACT.Abs_reciprocal_sqrt, bias=tiny[:])
 
         def st_n(u):
             nc.vector.tensor_tensor(out=nt("n_t", u)[:], in0=T["n2T", u][:], in1=T["rho", u][:], op=ALU.mult)
 
-        def st_w0(u):
-            nc.vector.scalar_tensor_tensor(
-                out=nt("w_t", u)[:], in0=T["n2T", u][:], scalar=1.0, in1=T["n_t", u][:], op0=ALU.subtract, op1=ALU.mult
-            )
-
         def st_x(u):
-            nc.gpsimd.tensor_scalar(out=nt("x_t", u)[:], in0=T["n_t", u][:], scalar1=1.0, scalar2=EPS, op0=ALU.mult, op1=ALU.add)
-
-        def st_w1(u):
-            if W1_ON_S:
-                nc.scalar.activation(out=T["w_t", u][:], in_=T["w_t", u][:], func=ACT.Identity, bias=m2eps[:])
-            else:
-                nc.gpsimd.tensor_scalar(
-                    out=T["w_t", u][:], in0=T["w_t", u][:], scalar1=1.0, scalar2=-2.0 * EPS, op0=ALU.mult, op1=ALU.add
-                )
+            nc.gpsimd.tensor_scalar(out=nt("x_t", u, 1)[:], in0=T["n_t", u][:], scalar1=1.0, scalar2=EPS, op0=ALU.mult, op1=ALU.add)
 
         def st_D(u):
             nc.vector.scalar_tensor_tensor(
                 out=nt("d_t", u)[:], in0=T["n2T", u][:], scalar=1.0, in1=T["x_t", u][:], op0=ALU.add, op1=ALU.mult
             )
 
-        def st_pw(u):
-            nc.vector.tensor_tensor(out=nt("pw", u)[:], in0=T["pT", u][:], in1=T["w_t", u][:], op=ALU.mult)
+        def st_w0(u):
+            nc.vector.scalar_tensor_tensor(
+                out=nt("w_t", u)[:], in0=T["n2T", u][:], scalar=1.0, in1=T["n_t", u][:], op0=ALU.subtract, op1=ALU.mult
+            )
 
         def st_R(u):
             nc.scalar.activation(out=nt("r_t", u)[:], in_=T["d_t", u][:], func=ACT.Abs_reciprocal_sqrt)
-            st_w1(u)
+            nc.scalar.activation(out=T["w_t", u][:], in_=T["w_t", u][:], func=ACT.Identity, bias=m2eps[:])
             nc.scalar.activation(out=T["r_t", u][:], in_=T["r_t", u][:], func=ACT.Square)
             nc.scalar.activation(out=nt("r2", u)[:], in_=T["r_t", u][:], func=ACT.Square)
+
+        def st_pw(u):
+            nc.vector.tensor_tensor(out=nt("pw", u)[:], in0=T["pT", u][:], in1=T["w_t", u][:], op=ALU.mult)
 
         def st_fT(u):
             nc.vector.tensor_tensor(out=nt("fT", u)[:], in0=T["n2T", u][:], in1=T["r_t", u][:], op=ALU.mult)
 
         def st_eT(u):
-            nc.gpsimd.tensor_tensor(out=T["pw", u][:], in0=T["pw", u][:], in1=T["r2", u][:], op=ALU.mult)
+            eng = nc.vector if u >= NU - 1 else nc.gpsimd
+            eng.tensor_tensor(out=T["pw", u][:], in0=T["pw", u][:], in1=T["r2", u][:], op=ALU.mult)
 
         def back(src, dst):
             for b in range(0, 512, 128):
@@ -264,48 +279,54 @@ def tile_primary_capsule_t_v_kernel(tc, X, weight, s, grad_out, out_0, out_1):
 
         def st_sub(u):
             c, tp = u // 2, u % 2
-            q, g = c // 2, c % 2
+            q, g = ORDER[c]
             h, qq = q // 2, q % 2
             if qq == 0 and tp == 0:
                 T["a", h, g] = stg.tile([P, 4, 2, 512], BF16, name="a_t", align_bytes=64)
-            nc.gpsimd.tensor_tensor(
+            eng = nc.vector if u >= NU - V_SUBS else nc.gpsimd
+            eng.tensor_tensor(
                 out=T["a", h, g][:, 2 * tp : 2 * tp + 2, :, qq * 256 : (qq + 1) * 256],
                 in0=T["fg", u][:],
                 in1=T["es", u][:],
                 op=ALU.subtract,
             )
             if qq == 1:
-                T["g2", u] = stg.tile([P, 2, 1024], BF16, name="g2", align_bytes=64)
+                if tp == 0:
+                    T["g2", c] = stg.tile([P, 4, 1024], BF16, name="g2", align_bytes=64)
                 for tl in range(2):
-                    later("PE", 0.45, lambda tl=tl: turn(u, tl))
+                    later("PE", 0.45, lambda tl=tl: turn(u, tl), 0, False, ("xt",))
             if tp == 1:
-                T["bt", c] = stg.tile([P, 2, 256, 4], BF16, name="bt", align_bytes=64)
-                for d in (1, 0):
-                    later("C", 0.9, lambda d=d: weave(c, d), 1, True)
+                if g == 0:
+                    T["bt", q] = stg.tile([P, 2, 2, 256, 4], BF16, name="bt", align_bytes=64)
+                for d in (1, 0) if c == 7 else (0, 1):
+                    later("C", 0.9, lambda d=d: weave(c, d), 0, c == 7)
 
         def weave(c, d):
-            q, g = c // 2, c % 2
+            q, g = ORDER[c]
             h, qq = q // 2, q % 2
-            cp(out=T["bt", c][:, d], in_=T["a", h, g][:, :, d, qq * 256 : (qq + 1) * 256].rearrange("p t i -> p i t"))
-            if d == 1:
-                later("V", 0.5, lambda: quant_b(c))
+            cp(out=T["bt", q][:, g, d], in_=T["a", h, g][:, :, d, qq * 256 : (qq + 1) * 256].rearrange("p t i -> p i t"))
+            if d == 1 and (g == 1 or q >= 2):
+                later("V", 0.95, lambda: quant_b(q, g), 1, c == 7)
 
-        def quant_b(c):
-            q, g = c // 2, c % 2
-            T["c1", c] = stg.tile([P, 512], U32, name="c1", bufs=4, align_bytes=64)
-            T["s1", c] = stg.tile([P, 512], U8, name="s1", bufs=4, align_bytes=64)
+        def quant_b(q, g):
+            if g == 0 or q < 2:
+                T["c1", q] = stg.tile([P, 1024], U32, name="c1", align_bytes=64)
+                T["s1", q] = stg.tile([P, 1024], U8, name="s1", align_bytes=64)
+            lo, hi = (0, 1024) if q < 2 else (g * 512, g * 512 + 512)
             nc.vector.quantize_mx(
-                out=T["c1", c][:].bitcast(E5), scales=T["s1", c][:], in_=T["bt", c][:].rearrange("p d i t -> p (d i t)")
+                out=T["c1", q][:, lo:hi].bitcast(E5),
+                scales=T["s1", q][:, lo:hi],
+                in_=T["bt", q][:].rearrange("p g d i t -> p (g d i t)")[:, 4 * lo : 4 * hi],
             )
             if g == 1:
-                later("PE", 0.9, lambda: mm_out1(q, 0))
-                if q == 3:
-                    later("PE", 0.9, lambda: mm_out1(q, 1))
+                for ib in (1, 0):
+                    later("PE", 0.9, lambda ib=ib: mm_out1(q, ib), 0, True, ("x", "acc"))
 
         spare = [(ps_a, "acc"), (ps_a, "acc"), (ps_r, "fp"), (ps_r, "eN"), (ps_n, "n2T"), (ps_n, "n2T")]
         n_acc = [0]
 
         def new_acc():
+            free["acc"] -= 1
             if not drain[0]:
                 return ps_a.tile([P, 512], F32, name="acc")
             n_acc[0] += 1
@@ -317,65 +338,63 @@ def tile_primary_capsule_t_v_kernel(tc, X, weight, s, grad_out, out_0, out_1):
             for g in range(2):
                 for d in range(2):
                     ox = (g * 2 + d) * 512
-                    oc = d * 256 + ib * 128
+                    oc = g * 512 + d * 256 + ib * 128
                     nc.tensor.matmul_mx(
                         out=acc[:],
-                        lhsT=T["c1", q * 2 + g][:, oc : oc + 128].bitcast(E5),
-                        lhsT_scale=T["s1", q * 2 + g][:, oc : oc + 128],
+                        lhsT=T["c1", q][:, oc : oc + 128].bitcast(E5),
+                        lhsT_scale=T["s1", q][:, oc : oc + 128],
                         rhs=xc[:, ox : ox + 512].bitcast(E4),
                         rhs_scale=xs[:, ox : ox + 512],
                         start=(g == 0 and d == 0),
                         stop=(g == 1 and d == 1),
                     )
-            o1 = stg.tile([P, 256, 4, 2], F32, name="o1")
-            for jh in range(2):
-                later("C", 0.9, lambda jh=jh: out1_copy(q, ib, acc, o1, jh), PE_LAG)
+            for jh in (1, 0) if q == 3 else (0, 1):
+                later("C", 0.9, lambda jh=jh: out1_copy(q, ib, acc, jh), 1, q == 3)
 
-        def out1_copy(q, ib, acc, o1, jh):
+        def out1_copy(q, ib, acc, jh):
+            o1 = stg.tile([P, 128, 4, 2], F32, name="o1", bufs=3)
             cp(
-                out=o1[:, jh * 128 : (jh + 1) * 128],
+                out=o1[:],
                 in_=acc[:, jh * 256 : (jh + 1) * 256].rearrange("p (j d) -> p j d", d=2).unsqueeze(2).to_broadcast([P, 128, 4, 2]),
             )
-            if q == 3:
-                nc.sync.dma_start(
-                    out=o1v[:, q * 2 + ib, jh * 1024 : (jh + 1) * 1024],
-                    in_=o1[:, jh * 128 : (jh + 1) * 128].rearrange("p j k d -> p (j k d)"),
-                )
-            elif jh == 1:
-                nc.sync.dma_start(out=o1v[:, q * 2 + ib, :], in_=o1[:].rearrange("p j k d -> p (j k d)"))
-                if ib == 0:
-                    later("PE", 0.9, lambda: mm_out1(q, 1), 0)
+            nc.sync.dma_start(out=o1v[:, q * 2 + ib, jh * 1024 : (jh + 1) * 1024], in_=o1[:].rearrange("p j k d -> p (j k d)"))
+            if jh == 1:
+                free["acc"] += 1
 
         def turn(u, tl):
             c, tp = u // 2, u % 2
-            q, g = c // 2, c % 2
+            q, g = ORDER[c]
+            free["xt"] -= 1
             xt = ps_x.tile([P, 512], F32, name="xt")
             for d in range(2):
                 aw = T["a", q // 2, g][:, 2 * tp + tl, d, :].bitcast(F32)
                 for w in range(2):
                     b = (d * 2 + w) * 128
                     nc.tensor.transpose(out=xt[:, b : b + 128], in_=aw[:, w:256:2], identity=ident[:])
-            later("C", 0.45, lambda: turn_copy(u, tl, xt), PE_LAG)
+            later("C", 0.45, lambda: turn_copy(u, tl, xt), 1)
 
         def turn_copy(u, tl, xt):
+            c, tp = u // 2, u % 2
             cp(
-                out=T["g2", u][:, tl].bitcast(F32).rearrange("p (d r w) -> p d r w", d=2, r=128, w=2),
+                out=T["g2", c][:, 2 * tp + tl].bitcast(F32).rearrange("p (d r w) -> p d r w", d=2, r=128, w=2),
                 in_=xt[:].rearrange("p (d w r) -> p d r w", d=2, w=2, r=128),
             )
-            if tl == 1:
-                later("V", 0.55, lambda: quant_i(u))
+            free["xt"] += 1
+            if tl == 1 and (tp == 1 or c == 7):
+                later("V", 0.95, lambda: quant_i(c, tp), 0 if drain[0] else 1)
 
-        def quant_i(u):
-            c, tp = u // 2, u % 2
-            q, g = c // 2, c % 2
+        def quant_i(c, tp):
+            q, g = ORDER[c]
             h = q // 2
-            o = (g * 4 + 2 * tp) * 256
+            lo, hi = (0, 4) if c < 7 else (2 * tp, 2 * tp + 2)
             nc.vector.quantize_mx(
-                out=c2[h][:, o : o + 512].bitcast(E5), scales=s2[h][:, o : o + 512], in_=T["g2", u][:].rearrange("p t w -> p (t w)")
+                out=c2[h][:, g * 1024 + lo * 256 : g * 1024 + hi * 256].bitcast(E5),
+                scales=s2[h][:, g * 1024 + lo * 256 : g * 1024 + hi * 256],
+                in_=T["g2", c][:, lo:hi].rearrange("p t w -> p (t w)"),
             )
             if h == 1:
-                for tl in range(2):
-                    later("PE", 0.9, lambda tl=tl: mm_out0(g, 2 * tp + tl), 1 + (0 if drain[0] else 2 * tl))
+                for t in range(lo, hi):
+                    later("PE", 0.9, lambda t=t: mm_out0(g, t), 0, False, ("w", "acc"))
 
         def mm_out0(g, t):
             acc = new_acc()
@@ -392,11 +411,12 @@ def tile_primary_capsule_t_v_kernel(tc, X, weight, s, grad_out, out_0, out_1):
                         start=(hh == 0 and d == 0),
                         stop=(hh == 1 and d == 1),
                     )
-            later("C", 0.45, lambda: out0_copy(g, t, acc), PE_LAG)
+            later("C", 0.45, lambda: out0_copy(g, t, acc), 1)
 
         def out0_copy(g, t, acc):
             o0 = stg.tile([P, 512], F32, name="o0", bufs=3)
             cp(out=o0[:], in_=acc[:])
+            free["acc"] += 1
             nc.sync.dma_start(out=o0v[:, g, t, :], in_=o0[:])
 
         def ok(u):
@@ -405,68 +425,80 @@ def tile_primary_capsule_t_v_kernel(tc, X, weight, s, grad_out, out_0, out_1):
         def left():
             return len(bg["C"]) + len(bg["V"]) + len(bg["W"]) + len(bg["PE"])
 
-        drain = [False]
-
-        def slot(bud_c, bud_v, bud_pe):
+        def slot():
             if drain[0]:
-                while len(bg["C"]) > 0 and run_bg("C", 0.1) > 0.0:
-                    side[0] = "V" if side[0] == "S" else "S"
-                side[0] = "S"
-                run_bg("W", 9.0, run_bg("V", 9.0))
-                run_bg("PE", 9.0)
+                moved = 1.0
+                while moved > 0.0:
+                    moved = run_bg("W", 9.0, run_bg("V", 9.0)) + run_bg("PE", 9.0)
+                    if run_bg("C", 0.1) > 0.0:
+                        moved += 1.0
+                        side[0] = "V" if side[0] == "S" else "S"
             else:
-                run_bg("C", bud_c)
-                run_bg("W", bud_v, run_bg("V", bud_v))
-                run_bg("PE", bud_pe)
+                run_bg("C", BUD_S if now[0] < NU else 9.0)
+                run_bg("W", BUD_V, run_bg("V", BUD_V))
+                run_bg("PE", BUD_PE)
 
-        load_chunk(0)
-        load_chunk(1)
-        x_load(0)
-        x_load(1)
-        load_chunk(2)
-        for d in range(2):
-            later("C", 0.95, lambda d=d: x_copy(0, d), 3)
-        st_sq(0)
-        st_gs(0)
-        st_n2T(0)
-        it = 0
-        while it < NU + 2 or left() > 0:
-            u = it
-            drain[0] = it >= NU
-            now[0] = 2 * it
-            if ok(u):
-                st_rho(u)
-                st_n(u)
-                st_x(u)
-            if ok(u + 1):
-                st_sq(u + 1)
-            if ok(u - 1):
-                st_fg(u - 1)
-            if ok(u):
-                st_pT(u)
-            if ok(u + 1):
-                st_n2T(u + 1)
-            if ok(u):
-                st_D(u)
-                st_w0(u)
-            if ok(u - 2):
-                st_sub(u - 2)
-            slot(BUD_SA, BUD_VA, BUD_PE)
-            if ok(u):
-                st_R(u)
-            if ok(u - 1):
-                st_es(u - 1)
-                if u % 2 == 0 and u // 2 + 2 < NU // 2:
-                    load_chunk(u // 2 + 2)
-            if ok(u):
-                st_pw(u)
-                st_fT(u)
-            if ok(u + 1):
-                st_gs(u + 1)
-            if ok(u):
-                st_eT(u)
-                st_fN(u)
-                st_eN(u)
-            now[0] = 2 * it + 1
-            slot(BUD_SB, BUD_VB, 0.0)
+        def one_round(it):
+            now[0] = it
+            if ok(it):
+                st_rho(it)
+            if ok(it - 2):
+                st_fg(it - 2)
+            if ok(it - 3):
+                st_sub(it - 3)
+            if it == NU + 2:
+                drain[0] = True
+                free["acc"] += 4
+            if ok(it - 1):
+                st_R(it - 1)
+            if ok(it):
+                st_n(it)
+            if ok(it - 1):
+                st_pT(it - 1)
+            if ok(it):
+                st_gs(it)
+            if ok(it - 2):
+                st_es(it - 2)
+                if it % 2 == 1 and (it - 3) // 2 + 3 < NU // 2:
+                    load_chunk((it - 3) // 2 + 3, (0, 4))
+            if ok(it - 1):
+                st_pw(it - 1)
+                st_fT(it - 1)
+            if ok(it + 1):
+                st_sq(it + 1)
+            if ok(it - 1):
+                st_fN(it - 1)
+            if ok(it + 1):
+                st_n2T(it + 1)
+            if ok(it):
+                st_x(it)
+            if it < LATE:
+                slot()
+            if ok(it):
+                st_D(it)
+                st_w0(it)
+            if ok(it - 1):
+                st_eT(it - 1)
+                st_eN(it - 1)
+            if it >= LATE:
+                slot()
+
+        def head():
+            load_chunk(0, (0, 2))
+            next_load()
+            load_chunk(0, (2, 4))
+            load_chunk(1, (0, 4))
+            next_load()
+            load_chunk(2, (0, 4))
+            w_half(0)
+            st_sq(0)
+            st_n2T(0)
+
+        with tc.manual_schedule():
+            head()
+            for it in range(CUT):
+                one_round(it)
+        it = CUT
+        while it < NU + 4 or left() > 0:
+            one_round(it)
             it += 1

@@ -8,497 +8,535 @@ BF16 = mybir.dt.bfloat16
 U32 = mybir.dt.uint32
 U8 = mybir.dt.uint8
 I32 = mybir.dt.int32
-E4 = mybir.dt.float8_e4m3fn_x4
-E5 = mybir.dt.float8_e5m2_x4
+E4M3 = mybir.dt.float8_e4m3fn_x4
+E5M2 = mybir.dt.float8_e5m2_x4
 ALU = mybir.AluOpType
 ACT = mybir.ActivationFunctionType
-AX = mybir.AxisListType
+AXIS = mybir.AxisListType
 
 P = 128
 EPS = 1e-8
 TINY = 1e-30
 FLOPS = 2 * 2 * 2 * 1024 * 1024 * 256
-NU = 16
-ORDER = ((0, 0), (0, 1), (1, 0), (1, 1), (2, 0), (2, 1), (3, 0), (3, 1))
-BUD_S = 2.6
-BUD_V = 1.6
-BUD_PE = 2.0
-XW_BUFS = 2
-W_LAG = 0
-V_SUBS = 2
-LATE = 14
-CUT = 15
+
+UNITS = 16
+LAST_CHUNK = UNITS // 2 - 1
+ROUNDS = UNITS + 3
+PINNED = 15
+SIDE_WORK_AT_THE_END_FROM = 14
+COPY_ROOM = 6
+VECTOR_ROOM = 4
+TENSOR_ROOM = 5
+ALL = 999
+SUBTRACT_ON_VECTOR_FROM = UNITS - 2
+E_ON_VECTOR_FROM = UNITS - 1
 
 
 def tile_primary_capsule_t_v_kernel(tc, X, weight, s, grad_out, out_0, out_1):
     nc = tc.nc
-    xv = X.rearrange("(g p t) j d -> p g (t j d)", g=2, p=P, t=4)
-    wv = weight.rearrange("(h p t) j k d -> p h t (j k d)", h=2, p=P, t=4)
-    sv = s.rearrange("(g p t) (q i) d -> p g t q (i d)", g=2, p=P, t=4, q=4)
-    gv = grad_out.rearrange("(g p t) (q i) d -> p g t q (i d)", g=2, p=P, t=4, q=4)
-    o0v = out_0.rearrange("(g p t) j d -> p g t (j d)", g=2, p=P, t=4)
-    o1v = out_1.rearrange("(m p) j k d -> p m (j k d)", p=P)
+    x_hbm = X.rearrange("(g p t) j d -> p g (t j d)", g=2, p=P, t=4)
+    w_hbm = weight.rearrange("(h p t) j k d -> p h t (j k d)", h=2, p=P, t=4)
+    s_hbm = s.rearrange("(g p t) (q i) d -> p g t q (i d)", g=2, p=P, t=4, q=4)
+    g_hbm = grad_out.rearrange("(g p t) (q i) d -> p g t q (i d)", g=2, p=P, t=4, q=4)
+    out_0_hbm = out_0.rearrange("(g p t) j d -> p g t (j d)", g=2, p=P, t=4)
+    out_1_hbm = out_1.rearrange("(m p) j k d -> p m (j k d)", p=P)
 
     with ExitStack() as ctx:
         const = ctx.enter_context(tc.tile_pool(name="const", bufs=1))
         keep = ctx.enter_context(tc.tile_pool(name="keep", bufs=1))
-        ld = ctx.enter_context(tc.tile_pool(name="ld", bufs=3))
+        loaded = ctx.enter_context(tc.tile_pool(name="loaded", bufs=3))
         wide = ctx.enter_context(tc.tile_pool(name="wide", bufs=2))
-        nar = ctx.enter_context(tc.tile_pool(name="nar", bufs=2))
-        stg = ctx.enter_context(tc.tile_pool(name="stg", bufs=2))
-        ps_n = ctx.enter_context(tc.psum_pool(name="ps_n", bufs=2))
-        ps_r = ctx.enter_context(tc.psum_pool(name="ps_r", bufs=1))
-        ps_x = ctx.enter_context(tc.psum_pool(name="ps_x", bufs=2))
-        ps_a = ctx.enter_context(tc.psum_pool(name="ps_a", bufs=2))
+        narrow = ctx.enter_context(tc.tile_pool(name="narrow", bufs=2))
+        staged = ctx.enter_context(tc.tile_pool(name="staged", bufs=2))
+        psum = ctx.enter_context(tc.psum_pool(name="psum", bufs=1))
 
-        ident = const.tile([P, P], F32, name="ident")
-        masks.make_identity(nc, ident[:])
+        identity = const.tile([P, P], F32, name="identity")
+        masks.make_identity(nc, identity[:])
         tiny = const.tile([P, 1], F32, name="tiny")
         nc.vector.memset(tiny[:], TINY)
-        m2eps = const.tile([P, 1], F32, name="m2eps")
-        nc.vector.memset(m2eps[:], -2.0 * EPS)
+        minus_2_eps = const.tile([P, 1], F32, name="minus_2_eps")
+        nc.vector.memset(minus_2_eps[:], -2.0 * EPS)
 
-        mg = keep.tile([P, 2, 256, 2, 4], BF16, name="mg", align_bytes=64)
-        nc.vector.memset(mg[:].rearrange("p d j e t -> p (d j e t)").bitcast(I32), 0)
-        xc = keep.tile([P, 2048], U32, name="xc", align_bytes=64)
-        xs = keep.tile([P, 2048], U8, name="xs", align_bytes=64)
-        wc = keep.tile([P, 2048], U32, name="wc", align_bytes=64)
-        ws = keep.tile([P, 2048], U8, name="ws", align_bytes=64)
-        c2 = {}
-        s2 = {}
+        masked = keep.tile([P, 2, 256, 2, 4], BF16, name="masked", align_bytes=64)
+        nc.vector.memset(masked[:].rearrange("p d j e t -> p (d j e t)").bitcast(I32), 0)
+        x_codes = keep.tile([P, 2048], U32, name="x_codes", align_bytes=64)
+        x_scales = keep.tile([P, 2048], U8, name="x_scales", align_bytes=64)
+        w_codes = keep.tile([P, 2048], U32, name="w_codes", align_bytes=64)
+        w_scales = keep.tile([P, 2048], U8, name="w_scales", align_bytes=64)
+        ds_T_codes = {}
+        ds_T_scales = {}
         for h in range(2):
-            c2[h] = keep.tile([P, 2048], U32, name="c2_%d" % h, align_bytes=64)
-            s2[h] = keep.tile([P, 2048], U8, name="s2_%d" % h, align_bytes=64)
+            ds_T_codes[h] = keep.tile([P, 2048], U32, name="ds_T_codes%d" % h, align_bytes=64)
+            ds_T_scales[h] = keep.tile([P, 2048], U8, name="ds_T_scales%d" % h, align_bytes=64)
 
-        T = {}
-        bg = {"C": [], "V": [], "W": [], "PE": []}
-        now = [0]
-        drain = [False]
-        side = ["S"]
+        tiles = {}
 
-        free = {"": 1, "x": 0, "w": 0, "xt": 2, "acc": 2}
+        todo = {"copy": [], "vector": [], "w_sum": [], "tensor": []}
+        this_round = [0]
+        at_the_end = [False]
+        copy_engine = ["scalar"]
+        there = {"x": 0, "w": 0, "turned": 2, "sum": 2}
+        free_banks = {"turned": ["turned0", "turned1"], "sum": ["sum0", "sum1"]}
 
-        def later(eng, cost, fn, delay=1, first=False, need=("",)):
-            if drain[0]:
-                delay = 0
+        def later(kind, size, piece, rounds=1, first=False, needs=()):
+            entry = (this_round[0] + (0 if at_the_end[0] else rounds), size, piece, needs)
             if first:
-                bg[eng].insert(0, (now[0] + delay, cost, fn, need))
+                todo[kind].insert(0, entry)
             else:
-                bg[eng].append((now[0] + delay, cost, fn, need))
+                todo[kind].append(entry)
 
-        def run_bg(eng, budget, spent=0.0):
+        def issue(kind, room, used=0):
             k = 0
-            while k < len(bg[eng]) and spent < budget:
-                if bg[eng][k][0] <= now[0] and all(free[r] > 0 for r in bg[eng][k][3]):
-                    piece = bg[eng].pop(k)
-                    spent += piece[1]
-                    piece[2]()
+            while k < len(todo[kind]) and used < room:
+                if todo[kind][k][0] <= this_round[0] and all(there[need] > 0 for need in todo[kind][k][3]):
+                    entry = todo[kind].pop(k)
+                    used += entry[1]
+                    entry[2]()
                 else:
                     k += 1
-            return spent
+            return used
 
-        def cp(out, in_):
-            if side[0] == "S":
+        def take_bank(kind):
+            there[kind] -= 1
+            name = free_banks[kind].pop(0)
+            return name, psum.tile([P, 512], F32, name=name)
+
+        def give_bank(kind, name):
+            there[kind] += 1
+            free_banks[kind].append(name)
+
+        def copy(out, in_):
+            if copy_engine[0] == "scalar":
                 nc.scalar.copy(out=out, in_=in_)
             else:
                 nc.vector.tensor_copy(out=out, in_=in_)
 
-        def load_chunk(c, parts):
-            q, g = ORDER[c]
-            if parts[0] == 0:
-                T["s", c] = ld.tile([P, 4, 512], F32, name="s_sb")
-                T["g", c] = ld.tile([P, 4, 512], BF16, name="g_sb")
-            a, b = parts
-            nc.sync.dma_start(out=T["s", c][:, a:b], in_=sv[:, g, a:b, q, :])
-            nc.sync.dma_start(out=T["g", c][:, a:b], in_=gv[:, g, a:b, q, :])
-
-        def quant_m(codes, scales, o):
-            nc.vector.quantize_mx(
-                out=codes[:, o : o + 1024].bitcast(E4),
-                scales=scales[:, o : o + 1024],
-                in_=mg[:].rearrange("p d j e t -> p (d j e t)"),
-            )
-
-        def x_load(g):
-            T["x", g] = ld.tile([P, 4096], BF16, name="xw_sb", bufs=XW_BUFS)
-            nc.sync.dma_start(out=T["x", g][:, 0:2048], in_=xv[:, g, :])
-
-        def w_load(h, jh):
-            T["w", h, jh] = ld.tile([P, 4096], BF16, name="xw_sb", bufs=XW_BUFS)
-            nc.sync.dma_start(
-                out=T["w", h, jh][:].rearrange("p (t w) -> p t w", t=4), in_=wv[:, h, :, jh * 1024 : (jh + 1) * 1024]
-            )
-
-        loads = [lambda: w_load(0, 0), lambda: w_load(0, 1), lambda: x_load(0), lambda: x_load(1), lambda: w_load(1, 0), lambda: w_load(1, 1)]
-
-        def next_load():
-            if len(loads) > 0:
-                loads.pop(0)()
-
-        def x_copy(g, d):
-            cp(
-                out=mg[:, d, :, d, :],
-                in_=T["x", g][:, 0:2048].rearrange("p (t j d) -> p d j t", t=4, j=256, d=2)[:, d],
-            )
-            if d == 1:
-                next_load()
-                later("V", 0.95, lambda: x_quant(g), 1, True)
-
-        def x_quant(g):
-            quant_m(xc, xs, g * 1024)
-            if g == 0:
-                for e in (1, 0):
-                    later("C", 0.95, lambda e=e: x_copy(1, e), 1, True)
+        def side_work():
+            if at_the_end[0]:
+                moved = 1
+                while moved > 0:
+                    moved = issue("vector", ALL) + issue("w_sum", ALL) + issue("tensor", ALL) + issue("copy", 1)
+                    copy_engine[0] = "vector" if copy_engine[0] == "scalar" else "scalar"
             else:
-                free["x"] = 1
-                w_half(1)
+                issue("copy", COPY_ROOM if this_round[0] < UNITS else ALL)
+                issue("w_sum", VECTOR_ROOM, issue("vector", VECTOR_ROOM))
+                issue("tensor", TENSOR_ROOM)
 
-        def w_half(h):
-            for jh in range(2):
-                for e in range(2):
-                    later("W", 1.75, lambda jh=jh, e=e: w_sum(h, jh, e), W_LAG if jh == 0 else 1)
-            later("W", 0.95, lambda: w_quant(h))
+        def load_chunk(c, t_lo, t_hi):
+            q, g = c // 2, c % 2
+            if t_lo == 0:
+                tiles["s", c] = loaded.tile([P, 4, 512], F32, name="s_chunk")
+                tiles["g", c] = loaded.tile([P, 4, 512], BF16, name="g_chunk")
+            nc.sync.dma_start(out=tiles["s", c][:, t_lo:t_hi], in_=s_hbm[:, g, t_lo:t_hi, q, :])
+            nc.sync.dma_start(out=tiles["g", c][:, t_lo:t_hi], in_=g_hbm[:, g, t_lo:t_hi, q, :])
 
-        def w_sum(h, jh, d):
+        def load_x(g):
+            tiles["x", g] = loaded.tile([P, 4096], BF16, name="x_or_w", bufs=2)
+            nc.sync.dma_start(out=tiles["x", g][:, 0:2048], in_=x_hbm[:, g, :])
+
+        def load_w(h, j_half):
+            tiles["w", h, j_half] = loaded.tile([P, 4096], BF16, name="x_or_w", bufs=2)
+            nc.sync.dma_start(
+                out=tiles["w", h, j_half][:].rearrange("p (t w) -> p t w", t=4),
+                in_=w_hbm[:, h, :, j_half * 1024 : (j_half + 1) * 1024],
+            )
+
+        x_w_loads = [
+            lambda: load_w(0, 0),
+            lambda: load_w(0, 1),
+            lambda: load_x(0),
+            lambda: load_x(1),
+            lambda: load_w(1, 0),
+            lambda: load_w(1, 1),
+        ]
+
+        def next_x_w_load():
+            if len(x_w_loads) > 0:
+                x_w_loads.pop(0)()
+
+        def quantize_masked(codes, scales, k_pass):
+            nc.vector.quantize_mx(
+                out=codes[:, k_pass * 1024 : (k_pass + 1) * 1024].bitcast(E4M3),
+                scales=scales[:, k_pass * 1024 : (k_pass + 1) * 1024],
+                in_=masked[:].rearrange("p d j e t -> p (d j e t)"),
+            )
+
+        def sum_w_half(h):
+            for j_half in range(2):
+                for d in range(2):
+                    later("w_sum", 4, lambda j_half=j_half, d=d: sum_w(h, j_half, d), 0 if j_half == 0 else 1)
+            later("w_sum", 2, lambda: quantize_w(h))
+
+        def sum_w(h, j_half, d):
             with nc.allow_low_precision(reason="the engine sums in float32 and rounds once to bfloat16"):
                 nc.vector.tensor_reduce(
-                    out=mg[:, d, jh * 128 : (jh + 1) * 128, d, :],
-                    in_=T["w", h, jh][:].rearrange("p (t j k d) -> p d j t k", t=4, j=128, k=4, d=2)[:, d],
-                    axis=AX.X,
+                    out=masked[:, d, j_half * 128 : (j_half + 1) * 128, d, :],
+                    in_=tiles["w", h, j_half][:].rearrange("p (t j k d) -> p d j t k", t=4, j=128, k=4, d=2)[:, d],
+                    axis=AXIS.X,
                     op=ALU.add,
                 )
             if d == 1:
-                next_load()
+                next_x_w_load()
 
-        def w_quant(h):
-            quant_m(wc, ws, h * 1024)
+        def quantize_w(h):
+            quantize_masked(w_codes, w_scales, h)
             if h == 0:
-                for e in (1, 0):
-                    later("C", 0.95, lambda e=e: x_copy(0, e), 1, True)
+                interleave_x_later(0)
             else:
-                free["w"] = 1
+                there["w"] = 1
 
-        def planes(u):
-            c, tp = u // 2, u % 2
-            s_pl = T["s", c][:, 2 * tp : 2 * tp + 2, :].rearrange("p t (i d) -> p t d i", d=2)
-            g_pl = T["g", c][:, 2 * tp : 2 * tp + 2, :].rearrange("p t (i d) -> p t d i", d=2)
-            return s_pl, g_pl
+        def interleave_x_later(g):
+            for d in (1, 0):
+                later("copy", 2, lambda d=d: interleave_x(g, d), 1, True)
 
-        def st_sq(u):
-            T["sq", u] = wide.tile([P, 2, 2, 256], F32, name="sq", bufs=1)
-            nc.scalar.activation(out=T["sq", u][:], in_=planes(u)[0], func=ACT.Square)
+        def interleave_x(g, d):
+            copy(
+                out=masked[:, d, :, d, :],
+                in_=tiles["x", g][:, 0:2048].rearrange("p (t j d) -> p d j t", t=4, j=256, d=2)[:, d],
+            )
+            if d == 1:
+                next_x_w_load()
+                later("vector", 2, lambda: quantize_x(g), 1, True)
 
-        def st_gs(u):
-            s_pl, g_pl = planes(u)
-            T["gs", u] = wide.tile([P, 2, 2, 256], F32, name="gs")
-            nc.gpsimd.tensor_tensor(out=T["gs", u][:], in0=g_pl, in1=s_pl, op=ALU.mult)
+        def quantize_x(g):
+            quantize_masked(x_codes, x_scales, g)
+            if g == 0:
+                interleave_x_later(1)
+            else:
+                there["x"] = 1
+                sum_w_half(1)
 
-        def add_over_d(src, dst):
-            for tl in range(2):
-                for ib in range(2):
-                    b = (tl * 2 + ib) * 128
+        def s_and_g(u):
+            c, pair = u // 2, u % 2
+            s_tdi = tiles["s", c][:, 2 * pair : 2 * pair + 2, :].rearrange("p t (i d) -> p t d i", d=2)
+            g_tdi = tiles["g", c][:, 2 * pair : 2 * pair + 2, :].rearrange("p t (i d) -> p t d i", d=2)
+            return s_tdi, g_tdi
+
+        def new_narrow(what, u, bufs=2):
+            tiles[what, u] = narrow.tile([P, 512], F32, name=what, bufs=bufs)
+            return tiles[what, u]
+
+        def square_s(u):
+            tiles["s_sq", u] = wide.tile([P, 2, 2, 256], F32, name="s_sq", bufs=1)
+            nc.scalar.activation(out=tiles["s_sq", u][:], in_=s_and_g(u)[0], func=ACT.Square)
+
+        def multiply_g_s(u):
+            s_tdi, g_tdi = s_and_g(u)
+            tiles["g_s", u] = wide.tile([P, 2, 2, 256], F32, name="g_s")
+            nc.gpsimd.tensor_tensor(out=tiles["g_s", u][:], in0=g_tdi, in1=s_tdi, op=ALU.mult)
+
+        def add_over_d_transposed(src, dst):
+            for t in range(2):
+                for block in range(2):
+                    col = (t * 2 + block) * 128
                     for d in range(2):
                         nc.tensor.matmul(
-                            out=dst[:, b : b + 128],
-                            lhsT=src[:, tl, d, ib * 128 : (ib + 1) * 128],
-                            rhs=ident[:],
+                            out=dst[:, col : col + 128],
+                            lhsT=src[:, t, d, block * 128 : (block + 1) * 128],
+                            rhs=identity[:],
                             is_transpose=True,
                             start=(d == 0),
                             stop=(d == 1),
                         )
 
-        def st_n2T(u):
-            T["n2T", u] = ps_n.tile([P, 512], F32, name="n2T")
-            add_over_d(T["sq", u], T["n2T", u])
+        def make_n2_T(u):
+            tiles["n2_T", u] = psum.tile([P, 512], F32, name="n2_T%d" % (u % 2))
+            add_over_d_transposed(tiles["s_sq", u], tiles["n2_T", u])
 
-        def st_pT(u):
-            T["pT", u] = ps_r.tile([P, 512], F32, name="fp")
-            add_over_d(T["gs", u], T["pT", u])
+        def make_p_T(u):
+            tiles["p_T", u] = psum.tile([P, 512], F32, name="p_T_or_f")
+            add_over_d_transposed(tiles["g_s", u], tiles["p_T", u])
 
-        def nt(name, u, bufs=2):
-            T[name, u] = nar.tile([P, 512], F32, name=name, bufs=bufs)
-            return T[name, u]
-
-        def st_rho(u):
-            nc.scalar.activation(out=nt("rho", u, 1)[:], in_=T["n2T", u][:], func=ACT.Abs_reciprocal_sqrt, bias=tiny[:])
-
-        def st_n(u):
-            nc.vector.tensor_tensor(out=nt("n_t", u)[:], in0=T["n2T", u][:], in1=T["rho", u][:], op=ALU.mult)
-
-        def st_x(u):
-            nc.gpsimd.tensor_scalar(out=nt("x_t", u, 1)[:], in0=T["n_t", u][:], scalar1=1.0, scalar2=EPS, op0=ALU.mult, op1=ALU.add)
-
-        def st_D(u):
-            nc.vector.scalar_tensor_tensor(
-                out=nt("d_t", u)[:], in0=T["n2T", u][:], scalar=1.0, in1=T["x_t", u][:], op0=ALU.add, op1=ALU.mult
+        def make_rho(u):
+            nc.scalar.activation(
+                out=new_narrow("rho", u, 1)[:], in_=tiles["n2_T", u][:], func=ACT.Abs_reciprocal_sqrt, bias=tiny[:]
             )
 
-        def st_w0(u):
-            nc.vector.scalar_tensor_tensor(
-                out=nt("w_t", u)[:], in0=T["n2T", u][:], scalar=1.0, in1=T["n_t", u][:], op0=ALU.subtract, op1=ALU.mult
+        def make_n(u):
+            nc.vector.tensor_tensor(
+                out=new_narrow("n_then_f_T", u)[:], in0=tiles["n2_T", u][:], in1=tiles["rho", u][:], op=ALU.mult
             )
 
-        def st_R(u):
-            nc.scalar.activation(out=nt("r_t", u)[:], in_=T["d_t", u][:], func=ACT.Abs_reciprocal_sqrt)
-            nc.scalar.activation(out=T["w_t", u][:], in_=T["w_t", u][:], func=ACT.Identity, bias=m2eps[:])
-            nc.scalar.activation(out=T["r_t", u][:], in_=T["r_t", u][:], func=ACT.Square)
-            nc.scalar.activation(out=nt("r2", u)[:], in_=T["r_t", u][:], func=ACT.Square)
+        def make_x(u):
+            nc.gpsimd.tensor_scalar(
+                out=new_narrow("x", u, 1)[:], in0=tiles["n_then_f_T", u][:], scalar1=1.0, scalar2=EPS, op0=ALU.mult, op1=ALU.add
+            )
 
-        def st_pw(u):
-            nc.vector.tensor_tensor(out=nt("pw", u)[:], in0=T["pT", u][:], in1=T["w_t", u][:], op=ALU.mult)
+        def make_D(u):
+            nc.vector.scalar_tensor_tensor(
+                out=new_narrow("D_then_R", u)[:],
+                in0=tiles["n2_T", u][:],
+                scalar=1.0,
+                in1=tiles["x", u][:],
+                op0=ALU.add,
+                op1=ALU.mult,
+            )
 
-        def st_fT(u):
-            nc.vector.tensor_tensor(out=nt("fT", u)[:], in0=T["n2T", u][:], in1=T["r_t", u][:], op=ALU.mult)
+        def make_n2_1_n(u):
+            nc.vector.scalar_tensor_tensor(
+                out=new_narrow("v", u)[:],
+                in0=tiles["n2_T", u][:],
+                scalar=1.0,
+                in1=tiles["n_then_f_T", u][:],
+                op0=ALU.subtract,
+                op1=ALU.mult,
+            )
 
-        def st_eT(u):
-            eng = nc.vector if u >= NU - 1 else nc.gpsimd
-            eng.tensor_tensor(out=T["pw", u][:], in0=T["pw", u][:], in1=T["r2", u][:], op=ALU.mult)
+        def scalar_steps(u):
+            d_then_r = tiles["D_then_R", u]
+            nc.scalar.activation(out=d_then_r[:], in_=d_then_r[:], func=ACT.Abs_reciprocal_sqrt)
+            nc.scalar.activation(out=tiles["v", u][:], in_=tiles["v", u][:], func=ACT.Identity, bias=minus_2_eps[:])
+            nc.scalar.activation(out=d_then_r[:], in_=d_then_r[:], func=ACT.Square)
+            nc.scalar.activation(out=new_narrow("R_squared", u)[:], in_=d_then_r[:], func=ACT.Square)
 
-        def back(src, dst):
-            for b in range(0, 512, 128):
-                nc.tensor.transpose(out=dst[:, b : b + 128], in_=src[:, b : b + 128], identity=ident[:])
+        def make_p_v(u):
+            nc.vector.tensor_tensor(
+                out=new_narrow("p_v_then_e_T", u)[:], in0=tiles["p_T", u][:], in1=tiles["v", u][:], op=ALU.mult
+            )
 
-        def st_fN(u):
-            T["fN", u] = ps_r.tile([P, 512], F32, name="fp")
-            back(T["fT", u], T["fN", u])
+        def make_f_T(u):
+            nc.vector.tensor_tensor(
+                out=tiles["n_then_f_T", u][:], in0=tiles["n2_T", u][:], in1=tiles["D_then_R", u][:], op=ALU.mult
+            )
 
-        def st_eN(u):
-            T["eN", u] = ps_r.tile([P, 512], F32, name="eN")
-            back(T["pw", u], T["eN", u])
+        def make_e_T(u):
+            engine = nc.vector if u >= E_ON_VECTOR_FROM else nc.gpsimd
+            engine.tensor_tensor(
+                out=tiles["p_v_then_e_T", u][:], in0=tiles["p_v_then_e_T", u][:], in1=tiles["R_squared", u][:], op=ALU.mult
+            )
 
-        def over_d(t):
-            return t[:].rearrange("p (t i) -> p t i", t=2).unsqueeze(2).to_broadcast([P, 2, 2, 256])
+        def transpose_back(src, dst):
+            for col in range(0, 512, 128):
+                nc.tensor.transpose(out=dst[:, col : col + 128], in_=src[:, col : col + 128], identity=identity[:])
 
-        def st_fg(u):
-            T["fg", u] = wide.tile([P, 2, 2, 256], F32, name="fg")
-            nc.vector.tensor_tensor(out=T["fg", u][:], in0=over_d(T["fN", u]), in1=planes(u)[1], op=ALU.mult)
+        def bring_f_back(u):
+            tiles["f", u] = psum.tile([P, 512], F32, name="p_T_or_f")
+            transpose_back(tiles["n_then_f_T", u], tiles["f", u])
 
-        def st_es(u):
-            T["es", u] = wide.tile([P, 2, 2, 256], F32, name="es")
-            nc.vector.tensor_tensor(out=T["es", u][:], in0=over_d(T["eN", u]), in1=planes(u)[0], op=ALU.mult)
+        def bring_e_back(u):
+            tiles["e", u] = psum.tile([P, 512], F32, name="e")
+            transpose_back(tiles["p_v_then_e_T", u], tiles["e", u])
 
-        def st_sub(u):
-            c, tp = u // 2, u % 2
-            q, g = ORDER[c]
-            h, qq = q // 2, q % 2
-            if qq == 0 and tp == 0:
-                T["a", h, g] = stg.tile([P, 4, 2, 512], BF16, name="a_t", align_bytes=64)
-            eng = nc.vector if u >= NU - V_SUBS else nc.gpsimd
-            eng.tensor_tensor(
-                out=T["a", h, g][:, 2 * tp : 2 * tp + 2, :, qq * 256 : (qq + 1) * 256],
-                in0=T["fg", u][:],
-                in1=T["es", u][:],
+        def for_both_d(bank):
+            return bank[:].rearrange("p (t i) -> p t i", t=2).unsqueeze(2).to_broadcast([P, 2, 2, 256])
+
+        def multiply_f_g(u):
+            tiles["f_g", u] = wide.tile([P, 2, 2, 256], F32, name="f_g")
+            nc.vector.tensor_tensor(out=tiles["f_g", u][:], in0=for_both_d(tiles["f", u]), in1=s_and_g(u)[1], op=ALU.mult)
+
+        def multiply_e_s(u):
+            tiles["e_s", u] = wide.tile([P, 2, 2, 256], F32, name="e_s")
+            nc.vector.tensor_tensor(out=tiles["e_s", u][:], in0=for_both_d(tiles["e", u]), in1=s_and_g(u)[0], op=ALU.mult)
+
+        def subtract(u):
+            c, pair = u // 2, u % 2
+            q, g = c // 2, c % 2
+            h, second_quarter = q // 2, q % 2
+            if second_quarter == 0 and pair == 0:
+                tiles["ds", h, g] = staged.tile([P, 4, 2, 512], BF16, name="ds", align_bytes=64)
+            engine = nc.vector if u >= SUBTRACT_ON_VECTOR_FROM else nc.gpsimd
+            engine.tensor_tensor(
+                out=tiles["ds", h, g][:, 2 * pair : 2 * pair + 2, :, second_quarter * 256 : (second_quarter + 1) * 256],
+                in0=tiles["f_g", u][:],
+                in1=tiles["e_s", u][:],
                 op=ALU.subtract,
             )
-            if qq == 1:
-                if tp == 0:
-                    T["g2", c] = stg.tile([P, 4, 1024], BF16, name="g2", align_bytes=64)
-                for tl in range(2):
-                    later("PE", 0.45, lambda tl=tl: turn(u, tl), 0, False, ("xt",))
-            if tp == 1:
+            if second_quarter == 1:
+                if pair == 0:
+                    tiles["ds_T", c] = staged.tile([P, 4, 1024], BF16, name="ds_T", align_bytes=64)
+                for t in (2 * pair, 2 * pair + 1):
+                    later("tensor", 1, lambda t=t: turn(c, t), 0, False, ("turned",))
+            if pair == 1:
                 if g == 0:
-                    T["bt", q] = stg.tile([P, 2, 2, 256, 4], BF16, name="bt", align_bytes=64)
-                for d in (1, 0) if c == 7 else (0, 1):
-                    later("C", 0.9, lambda d=d: weave(c, d), 0, c == 7)
+                    tiles["ds_woven", q] = staged.tile([P, 2, 2, 256, 4], BF16, name="ds_woven", align_bytes=64)
+                if c == LAST_CHUNK:
+                    for d in (1, 0):
+                        later("copy", 2, lambda d=d: weave(c, d), 0, True)
+                else:
+                    for d in (0, 1):
+                        later("copy", 2, lambda d=d: weave(c, d), 0)
 
         def weave(c, d):
-            q, g = ORDER[c]
-            h, qq = q // 2, q % 2
-            cp(out=T["bt", q][:, g, d], in_=T["a", h, g][:, :, d, qq * 256 : (qq + 1) * 256].rearrange("p t i -> p i t"))
+            q, g = c // 2, c % 2
+            h, second_quarter = q // 2, q % 2
+            copy(
+                out=tiles["ds_woven", q][:, g, d],
+                in_=tiles["ds", h, g][:, :, d, second_quarter * 256 : (second_quarter + 1) * 256].rearrange("p t i -> p i t"),
+            )
             if d == 1 and (g == 1 or q >= 2):
-                later("V", 0.95, lambda: quant_b(q, g), 1, c == 7)
+                later("vector", 2, lambda: quantize_along_b(q, g), 1, c == LAST_CHUNK)
 
-        def quant_b(q, g):
+        def quantize_along_b(q, g):
             if g == 0 or q < 2:
-                T["c1", q] = stg.tile([P, 1024], U32, name="c1", align_bytes=64)
-                T["s1", q] = stg.tile([P, 1024], U8, name="s1", align_bytes=64)
+                tiles["ds_codes", q] = staged.tile([P, 1024], U32, name="ds_codes", align_bytes=64)
+                tiles["ds_scales", q] = staged.tile([P, 1024], U8, name="ds_scales", align_bytes=64)
             lo, hi = (0, 1024) if q < 2 else (g * 512, g * 512 + 512)
             nc.vector.quantize_mx(
-                out=T["c1", q][:, lo:hi].bitcast(E5),
-                scales=T["s1", q][:, lo:hi],
-                in_=T["bt", q][:].rearrange("p g d i t -> p (g d i t)")[:, 4 * lo : 4 * hi],
+                out=tiles["ds_codes", q][:, lo:hi].bitcast(E5M2),
+                scales=tiles["ds_scales", q][:, lo:hi],
+                in_=tiles["ds_woven", q][:].rearrange("p g d i t -> p (g d i t)")[:, 4 * lo : 4 * hi],
             )
             if g == 1:
-                for ib in (1, 0):
-                    later("PE", 0.9, lambda ib=ib: mm_out1(q, ib), 0, True, ("x", "acc"))
+                for block in (1, 0):
+                    later("tensor", 2, lambda block=block: multiply_out_1(q, block), 0, True, ("x", "sum"))
 
-        spare = [(ps_a, "acc"), (ps_a, "acc"), (ps_r, "fp"), (ps_r, "eN"), (ps_n, "n2T"), (ps_n, "n2T")]
-        n_acc = [0]
-
-        def new_acc():
-            free["acc"] -= 1
-            if not drain[0]:
-                return ps_a.tile([P, 512], F32, name="acc")
-            n_acc[0] += 1
-            pool, name = spare[n_acc[0] % len(spare)]
-            return pool.tile([P, 512], F32, name=name)
-
-        def mm_out1(q, ib):
-            acc = new_acc()
+        def multiply_out_1(q, block):
+            bank, acc = take_bank("sum")
             for g in range(2):
                 for d in range(2):
-                    ox = (g * 2 + d) * 512
-                    oc = g * 512 + d * 256 + ib * 128
+                    ds_col = g * 512 + d * 256 + block * 128
+                    x_col = (g * 2 + d) * 512
                     nc.tensor.matmul_mx(
                         out=acc[:],
-                        lhsT=T["c1", q][:, oc : oc + 128].bitcast(E5),
-                        lhsT_scale=T["s1", q][:, oc : oc + 128],
-                        rhs=xc[:, ox : ox + 512].bitcast(E4),
-                        rhs_scale=xs[:, ox : ox + 512],
+                        lhsT=tiles["ds_codes", q][:, ds_col : ds_col + 128].bitcast(E5M2),
+                        lhsT_scale=tiles["ds_scales", q][:, ds_col : ds_col + 128],
+                        rhs=x_codes[:, x_col : x_col + 512].bitcast(E4M3),
+                        rhs_scale=x_scales[:, x_col : x_col + 512],
                         start=(g == 0 and d == 0),
                         stop=(g == 1 and d == 1),
                     )
-            for jh in (1, 0) if q == 3 else (0, 1):
-                later("C", 0.9, lambda jh=jh: out1_copy(q, ib, acc, jh), 1, q == 3)
+            if q == 3:
+                for j_half in (1, 0):
+                    later("copy", 2, lambda j_half=j_half: store_out_1(q, block, j_half, acc, bank), 1, True)
+            else:
+                for j_half in (0, 1):
+                    later("copy", 2, lambda j_half=j_half: store_out_1(q, block, j_half, acc, bank), 1)
 
-        def out1_copy(q, ib, acc, jh):
-            o1 = stg.tile([P, 128, 4, 2], F32, name="o1", bufs=3)
-            cp(
-                out=o1[:],
-                in_=acc[:, jh * 256 : (jh + 1) * 256].rearrange("p (j d) -> p j d", d=2).unsqueeze(2).to_broadcast([P, 128, 4, 2]),
+        def store_out_1(q, block, j_half, acc, bank):
+            repeated = staged.tile([P, 128, 4, 2], F32, name="repeated", bufs=3)
+            copy(
+                out=repeated[:],
+                in_=acc[:, j_half * 256 : (j_half + 1) * 256]
+                .rearrange("p (j d) -> p j d", d=2)
+                .unsqueeze(2)
+                .to_broadcast([P, 128, 4, 2]),
             )
-            nc.sync.dma_start(out=o1v[:, q * 2 + ib, jh * 1024 : (jh + 1) * 1024], in_=o1[:].rearrange("p j k d -> p (j k d)"))
-            if jh == 1:
-                free["acc"] += 1
+            nc.sync.dma_start(
+                out=out_1_hbm[:, q * 2 + block, j_half * 1024 : (j_half + 1) * 1024],
+                in_=repeated[:].rearrange("p j k d -> p (j k d)"),
+            )
+            if j_half == 1:
+                give_bank("sum", bank)
 
-        def turn(u, tl):
-            c, tp = u // 2, u % 2
-            q, g = ORDER[c]
-            free["xt"] -= 1
-            xt = ps_x.tile([P, 512], F32, name="xt")
+        def turn(c, t):
+            q, g = c // 2, c % 2
+            bank, turned = take_bank("turned")
             for d in range(2):
-                aw = T["a", q // 2, g][:, 2 * tp + tl, d, :].bitcast(F32)
+                words = tiles["ds", q // 2, g][:, t, d, :].bitcast(F32)
                 for w in range(2):
-                    b = (d * 2 + w) * 128
-                    nc.tensor.transpose(out=xt[:, b : b + 128], in_=aw[:, w:256:2], identity=ident[:])
-            later("C", 0.45, lambda: turn_copy(u, tl, xt), 1)
+                    col = (d * 2 + w) * 128
+                    nc.tensor.transpose(out=turned[:, col : col + 128], in_=words[:, w:256:2], identity=identity[:])
+            later("copy", 1, lambda: gather_turned(c, t, turned, bank), 1)
 
-        def turn_copy(u, tl, xt):
-            c, tp = u // 2, u % 2
-            cp(
-                out=T["g2", c][:, 2 * tp + tl].bitcast(F32).rearrange("p (d r w) -> p d r w", d=2, r=128, w=2),
-                in_=xt[:].rearrange("p (d w r) -> p d r w", d=2, w=2, r=128),
+        def gather_turned(c, t, turned, bank):
+            copy(
+                out=tiles["ds_T", c][:, t].bitcast(F32).rearrange("p (d r w) -> p d r w", d=2, r=128, w=2),
+                in_=turned[:].rearrange("p (d w r) -> p d r w", d=2, w=2, r=128),
             )
-            free["xt"] += 1
-            if tl == 1 and (tp == 1 or c == 7):
-                later("V", 0.95, lambda: quant_i(c, tp), 0 if drain[0] else 1)
+            give_bank("turned", bank)
+            if t == 3 or (t == 1 and c >= LAST_CHUNK - 1):
+                later("vector", 2, lambda: quantize_along_i(c, t), 1)
 
-        def quant_i(c, tp):
-            q, g = ORDER[c]
+        def quantize_along_i(c, t_last):
+            q, g = c // 2, c % 2
             h = q // 2
-            lo, hi = (0, 4) if c < 7 else (2 * tp, 2 * tp + 2)
+            t_first = 0 if c < LAST_CHUNK - 1 else t_last - 1
+            lo, hi = g * 1024 + t_first * 256, g * 1024 + (t_last + 1) * 256
             nc.vector.quantize_mx(
-                out=c2[h][:, g * 1024 + lo * 256 : g * 1024 + hi * 256].bitcast(E5),
-                scales=s2[h][:, g * 1024 + lo * 256 : g * 1024 + hi * 256],
-                in_=T["g2", c][:, lo:hi].rearrange("p t w -> p (t w)"),
+                out=ds_T_codes[h][:, lo:hi].bitcast(E5M2),
+                scales=ds_T_scales[h][:, lo:hi],
+                in_=tiles["ds_T", c][:, t_first : t_last + 1].rearrange("p t w -> p (t w)"),
             )
             if h == 1:
-                for t in range(lo, hi):
-                    later("PE", 0.9, lambda t=t: mm_out0(g, t), 0, False, ("w", "acc"))
+                for t in range(t_first, t_last + 1):
+                    later("tensor", 2, lambda t=t: multiply_out_0(g, t), 0, False, ("w", "sum"))
 
-        def mm_out0(g, t):
-            acc = new_acc()
-            o = (g * 4 + t) * 256
-            for hh in range(2):
+        def multiply_out_0(g, t):
+            bank, acc = take_bank("sum")
+            for h in range(2):
                 for d in range(2):
-                    ow = (hh * 2 + d) * 512
+                    ds_col = (g * 4 + t) * 256 + d * 128
+                    w_col = (h * 2 + d) * 512
                     nc.tensor.matmul_mx(
                         out=acc[:],
-                        lhsT=c2[hh][:, o + d * 128 : o + (d + 1) * 128].bitcast(E5),
-                        lhsT_scale=s2[hh][:, o + d * 128 : o + (d + 1) * 128],
-                        rhs=wc[:, ow : ow + 512].bitcast(E4),
-                        rhs_scale=ws[:, ow : ow + 512],
-                        start=(hh == 0 and d == 0),
-                        stop=(hh == 1 and d == 1),
+                        lhsT=ds_T_codes[h][:, ds_col : ds_col + 128].bitcast(E5M2),
+                        lhsT_scale=ds_T_scales[h][:, ds_col : ds_col + 128],
+                        rhs=w_codes[:, w_col : w_col + 512].bitcast(E4M3),
+                        rhs_scale=w_scales[:, w_col : w_col + 512],
+                        start=(h == 0 and d == 0),
+                        stop=(h == 1 and d == 1),
                     )
-            later("C", 0.45, lambda: out0_copy(g, t, acc), 1)
+            later("copy", 1, lambda: store_out_0(g, t, acc, bank), 1)
 
-        def out0_copy(g, t, acc):
-            o0 = stg.tile([P, 512], F32, name="o0", bufs=3)
-            cp(out=o0[:], in_=acc[:])
-            free["acc"] += 1
-            nc.sync.dma_start(out=o0v[:, g, t, :], in_=o0[:])
-
-        def ok(u):
-            return 0 <= u < NU
-
-        def left():
-            return len(bg["C"]) + len(bg["V"]) + len(bg["W"]) + len(bg["PE"])
-
-        def slot():
-            if drain[0]:
-                moved = 1.0
-                while moved > 0.0:
-                    moved = run_bg("W", 9.0, run_bg("V", 9.0)) + run_bg("PE", 9.0)
-                    if run_bg("C", 0.1) > 0.0:
-                        moved += 1.0
-                        side[0] = "V" if side[0] == "S" else "S"
-            else:
-                run_bg("C", BUD_S if now[0] < NU else 9.0)
-                run_bg("W", BUD_V, run_bg("V", BUD_V))
-                run_bg("PE", BUD_PE)
-
-        def one_round(it):
-            now[0] = it
-            if ok(it):
-                st_rho(it)
-            if ok(it - 2):
-                st_fg(it - 2)
-            if ok(it - 3):
-                st_sub(it - 3)
-            if it == NU + 2:
-                drain[0] = True
-                free["acc"] += 4
-            if ok(it - 1):
-                st_R(it - 1)
-            if ok(it):
-                st_n(it)
-            if ok(it - 1):
-                st_pT(it - 1)
-            if ok(it):
-                st_gs(it)
-            if ok(it - 2):
-                st_es(it - 2)
-                if it % 2 == 1 and (it - 3) // 2 + 3 < NU // 2:
-                    load_chunk((it - 3) // 2 + 3, (0, 4))
-            if ok(it - 1):
-                st_pw(it - 1)
-                st_fT(it - 1)
-            if ok(it + 1):
-                st_sq(it + 1)
-            if ok(it - 1):
-                st_fN(it - 1)
-            if ok(it + 1):
-                st_n2T(it + 1)
-            if ok(it):
-                st_x(it)
-            if it < LATE:
-                slot()
-            if ok(it):
-                st_D(it)
-                st_w0(it)
-            if ok(it - 1):
-                st_eT(it - 1)
-                st_eN(it - 1)
-            if it >= LATE:
-                slot()
+        def store_out_0(g, t, acc, bank):
+            rows = staged.tile([P, 512], F32, name="rows", bufs=3)
+            copy(out=rows[:], in_=acc[:])
+            give_bank("sum", bank)
+            nc.sync.dma_start(out=out_0_hbm[:, g, t, :], in_=rows[:])
 
         def head():
-            load_chunk(0, (0, 2))
-            next_load()
-            load_chunk(0, (2, 4))
-            load_chunk(1, (0, 4))
-            next_load()
-            load_chunk(2, (0, 4))
-            w_half(0)
-            st_sq(0)
-            st_n2T(0)
+            load_chunk(0, 0, 2)
+            next_x_w_load()
+            load_chunk(0, 2, 4)
+            load_chunk(1, 0, 4)
+            next_x_w_load()
+            load_chunk(2, 0, 4)
+            sum_w_half(0)
+            square_s(0)
+            make_n2_T(0)
+
+        def one_round(r):
+            def unit(u):
+                return 0 <= u < UNITS
+
+            this_round[0] = r
+            if unit(r):
+                make_rho(r)
+            if unit(r - 2):
+                multiply_f_g(r - 2)
+            if unit(r - 3):
+                subtract(r - 3)
+                if r - 3 == UNITS - 1:
+                    at_the_end[0] = True
+                    for name in ("p_T_or_f", "e", "n2_T0", "n2_T1"):
+                        give_bank("sum", name)
+            if unit(r - 1):
+                scalar_steps(r - 1)
+            if unit(r):
+                make_n(r)
+            if unit(r - 1):
+                make_p_T(r - 1)
+            if unit(r):
+                multiply_g_s(r)
+            if unit(r - 2):
+                multiply_e_s(r - 2)
+                if r % 2 == 1 and (r - 3) // 2 + 3 <= LAST_CHUNK:
+                    load_chunk((r - 3) // 2 + 3, 0, 4)
+            if unit(r - 1):
+                make_p_v(r - 1)
+                make_f_T(r - 1)
+            if unit(r + 1):
+                square_s(r + 1)
+            if unit(r - 1):
+                bring_f_back(r - 1)
+            if unit(r + 1):
+                make_n2_T(r + 1)
+            if unit(r):
+                make_x(r)
+            if r < SIDE_WORK_AT_THE_END_FROM:
+                side_work()
+            if unit(r):
+                make_D(r)
+                make_n2_1_n(r)
+            if unit(r - 1):
+                make_e_T(r - 1)
+                bring_e_back(r - 1)
+            if r >= SIDE_WORK_AT_THE_END_FROM:
+                side_work()
 
         with tc.manual_schedule():
             head()
-            for it in range(CUT):
-                one_round(it)
-        it = CUT
-        while it < NU + 4 or left() > 0:
-            one_round(it)
-            it += 1
+            for r in range(PINNED):
+                one_round(r)
+        for r in range(PINNED, ROUNDS):
+            one_round(r)

@@ -26,7 +26,7 @@ PINNED = 15
 SIDE_WORK_AT_THE_END_FROM = 14
 COPY_ROOM = 6
 VECTOR_ROOM = 4
-TENSOR_ROOM = 5
+TENSOR_ROOM = 3
 ALL = 999
 SUBTRACT_ON_VECTOR_FROM = UNITS - 2
 E_ON_VECTOR_FROM = UNITS - 1
@@ -54,8 +54,6 @@ def tile_primary_capsule_t_v_kernel(tc, X, weight, s, grad_out, out_0, out_1):
         masks.make_identity(nc, identity[:])
         tiny = const.tile([P, 1], F32, name="tiny")
         nc.vector.memset(tiny[:], TINY)
-        minus_2_eps = const.tile([P, 1], F32, name="minus_2_eps")
-        nc.vector.memset(minus_2_eps[:], -2.0 * EPS)
 
         masked = keep.tile([P, 2, 256, 2, 4], BF16, name="masked", align_bytes=64)
         nc.vector.memset(masked[:].rearrange("p d j e t -> p (d j e t)").bitcast(I32), 0)
@@ -119,7 +117,7 @@ def tile_primary_capsule_t_v_kernel(tc, X, weight, s, grad_out, out_0, out_1):
                     copy_engine[0] = "vector" if copy_engine[0] == "scalar" else "scalar"
             else:
                 issue("copy", COPY_ROOM if this_round[0] < UNITS else ALL)
-                issue("w_sum", VECTOR_ROOM, issue("vector", VECTOR_ROOM))
+                issue("w_sum", 1, issue("vector", VECTOR_ROOM))
                 issue("tensor", TENSOR_ROOM)
 
         def load_chunk(c, t_lo, t_hi):
@@ -272,9 +270,9 @@ def tile_primary_capsule_t_v_kernel(tc, X, weight, s, grad_out, out_0, out_1):
                 op1=ALU.mult,
             )
 
-        def make_n2_1_n(u):
+        def make_n3_minus_n(u):
             nc.vector.scalar_tensor_tensor(
-                out=new_narrow("v", u)[:],
+                out=new_narrow("n3_minus_n", u)[:],
                 in0=tiles["n2_T", u][:],
                 scalar=1.0,
                 in1=tiles["n_then_f_T", u][:],
@@ -285,13 +283,17 @@ def tile_primary_capsule_t_v_kernel(tc, X, weight, s, grad_out, out_0, out_1):
         def scalar_steps(u):
             d_then_r = tiles["D_then_R", u]
             nc.scalar.activation(out=d_then_r[:], in_=d_then_r[:], func=ACT.Abs_reciprocal_sqrt)
-            nc.scalar.activation(out=tiles["v", u][:], in_=tiles["v", u][:], func=ACT.Identity, bias=minus_2_eps[:])
             nc.scalar.activation(out=d_then_r[:], in_=d_then_r[:], func=ACT.Square)
             nc.scalar.activation(out=new_narrow("R_squared", u)[:], in_=d_then_r[:], func=ACT.Square)
 
         def make_p_v(u):
-            nc.vector.tensor_tensor(
-                out=new_narrow("p_v_then_e_T", u)[:], in0=tiles["p_T", u][:], in1=tiles["v", u][:], op=ALU.mult
+            nc.vector.scalar_tensor_tensor(
+                out=new_narrow("p_v_then_e_T", u)[:],
+                in0=tiles["n3_minus_n", u][:],
+                scalar=2.0 * EPS,
+                in1=tiles["p_T", u][:],
+                op0=ALU.subtract,
+                op1=ALU.mult,
             )
 
         def make_f_T(u):
@@ -527,7 +529,7 @@ def tile_primary_capsule_t_v_kernel(tc, X, weight, s, grad_out, out_0, out_1):
                 side_work()
             if unit(r):
                 make_D(r)
-                make_n2_1_n(r)
+                make_n3_minus_n(r)
             if unit(r - 1):
                 make_e_T(r - 1)
                 bring_e_back(r - 1)

@@ -362,8 +362,10 @@ def tile_primary_capsule_t_v_kernel(tc, X, weight, s, grad_out, out_0, out_1):
             q, g = c // 2, c % 2
             h, second_quarter = q // 2, q % 2
             copy(
-                out=tiles["ds_woven", q][:, g, d],
-                in_=tiles["ds", h, g][:, :, d, second_quarter * 256 : (second_quarter + 1) * 256].rearrange("p t i -> p i t"),
+                out=tiles["ds_woven", q][:, g, d].rearrange("p (c i) t -> p c t i", i=4),
+                in_=tiles["ds", h, g][:, :, d, second_quarter * 256 : (second_quarter + 1) * 256].rearrange(
+                    "p t (c i) -> p c t i", i=4
+                ),
             )
             if d == 1 and (g == 1 or q >= 2):
                 later("vector", 2, lambda: quantize_along_b(q, g), 1, c == LAST_CHUNK)

from contextlib import ExitStack

import concourse.masks as masks
import concourse.mybir as mybir

F32 = mybir.dt.float32
BF16 = mybir.dt.bfloat16
U32 = mybir.dt.uint32
U8 = mybir.dt.uint8
I32 = mybir.dt.int32
E4M3 = mybir.dt.float8_e4m3fn_x4
E5M2 = mybir.dt.float8_e5m2_x4
ALU = mybir.AluOpType
ACT = mybir.ActivationFunctionType
AXIS = mybir.AxisListType

P = 128
EPS = 1e-8
TINY = 1e-30
FLOPS = 2 * 2 * 2 * 1024 * 1024 * 256

UNITS = 16
LAST_CHUNK = UNITS // 2 - 1
ROUNDS = UNITS + 3
PINNED = 15
SIDE_WORK_AT_THE_END_FROM = 14
COPY_ROOM = 6
VECTOR_ROOM = 4
TENSOR_ROOM = 3
ALL = 999
SUBTRACT_ON_VECTOR_FROM = UNITS - 2
E_ON_VECTOR_FROM = UNITS - 1


def tile_primary_capsule_t_v_kernel(tc, X, weight, s, grad_out, out_0, out_1):
    nc = tc.nc
    x_hbm = X.rearrange("(g p t) j d -> p g (t j d)", g=2, p=P, t=4)
    w_hbm = weight.rearrange("(h p t) j k d -> p h t (j k d)", h=2, p=P, t=4)
    s_hbm = s.rearrange("(g p t) (q i) d -> p g t q (i d)", g=2, p=P, t=4, q=4)
    g_hbm = grad_out.rearrange("(g p t) (q i) d -> p g t q (i d)", g=2, p=P, t=4, q=4)
    out_0_hbm = out_0.rearrange("(g p t) j d -> p g t (j d)", g=2, p=P, t=4)
    out_1_hbm = out_1.rearrange("(m p) j k d -> p m (j k d)", p=P)

    with ExitStack() as ctx:
        const = ctx.enter_context(tc.tile_pool(name="const", bufs=1))
        keep = ctx.enter_context(tc.tile_pool(name="keep", bufs=1))
        loaded = ctx.enter_context(tc.tile_pool(name="loaded", bufs=3))
        wide = ctx.enter_context(tc.tile_pool(name="wide", bufs=2))
        narrow = ctx.enter_context(tc.tile_pool(name="narrow", bufs=2))
        staged = ctx.enter_context(tc.tile_pool(name="staged", bufs=2))
        psum = ctx.enter_context(tc.psum_pool(name="psum", bufs=1))

        identity = const.tile([P, P], F32, name="identity")
        masks.make_identity(nc, identity[:])
        tiny = const.tile([P, 1], F32, name="tiny")
        nc.vector.memset(tiny[:], TINY)

        masked = keep.tile([P, 2, 256, 2, 4], BF16, name="masked", align_bytes=64)
        nc.vector.memset(masked[:].rearrange("p d j e t -> p (d j e t)").bitcast(I32), 0)
        x_codes = keep.tile([P, 2048], U32, name="x_codes", align_bytes=64)
        x_scales = keep.tile([P, 2048], U8, name="x_scales", align_bytes=64)
        w_codes = keep.tile([P, 2048], U32, name="w_codes", align_bytes=64)
        w_scales = keep.tile([P, 2048], U8, name="w_scales", align_bytes=64)
        ds_T_codes = {}
        ds_T_scales = {}
        for h in range(2):
            ds_T_codes[h] = keep.tile([P, 2048], U32, name="ds_T_codes%d" % h, align_bytes=64)
            ds_T_scales[h] = keep.tile([P, 2048], U8, name="ds_T_scales%d" % h, align_bytes=64)

        tiles = {}

        todo = {"copy": [], "vector": [], "w_sum": [], "tensor": []}
        this_round = [0]
        at_the_end = [False]
        copy_engine = ["scalar"]
        there = {"x": 0, "w": 0, "turned": 2, "sum": 2}
        free_banks = {"turned": ["turned0", "turned1"], "sum": ["sum0", "sum1"]}

        def later(kind, size, piece, rounds=1, first=False, needs=()):
            entry = (this_round[0] + (0 if at_the_end[0] else rounds), size, piece, needs)
            if first:
                todo[kind].insert(0, entry)
            else:
                todo[kind].append(entry)

        def issue(kind, room, used=0):
            k = 0
            while k < len(todo[kind]) and used < room:
                if todo[kind][k][0] <= this_round[0] and all(there[need] > 0 for need in todo[kind][k][3]):
                    entry = todo[kind].pop(k)
                    used += entry[1]
                    entry[2]()
                else:
                    k += 1
            return used

        def take_bank(kind):
            there[kind] -= 1
            name = free_banks[kind].pop(0)
            return name, psum.tile([P, 512], F32, name=name)

        def give_bank(kind, name):
            there[kind] += 1
            free_banks[kind].append(name)

        def copy(out, in_):
            if copy_engine[0] == "scalar":
                nc.scalar.copy(out=out, in_=in_)
            else:
                nc.vector.tensor_copy(out=out, in_=in_)

        def side_work():
            if at_the_end[0]:
                moved = 1
                while moved > 0:
                    moved = issue("vector", ALL) + issue("w_sum", ALL) + issue("tensor", ALL) + issue("copy", 1)
                    copy_engine[0] = "vector" if copy_engine[0] == "scalar" else "scalar"
            else:
                issue("copy", COPY_ROOM if this_round[0] < UNITS else ALL)
                issue("w_sum", 1, issue("vector", VECTOR_ROOM))
                issue("tensor", TENSOR_ROOM)

        def load_chunk(c, t_lo, t_hi):
            q, g = c // 2, c % 2
            if t_lo == 0:
                tiles["s", c] = loaded.tile([P, 4, 512], F32, name="s_chunk")
                tiles["g", c] = loaded.tile([P, 4, 512], BF16, name="g_chunk")
            nc.sync.dma_start(out=tiles["s", c][:, t_lo:t_hi], in_=s_hbm[:, g, t_lo:t_hi, q, :])
            nc.sync.dma_start(out=tiles["g", c][:, t_lo:t_hi], in_=g_hbm[:, g, t_lo:t_hi, q, :])

        def load_x(g):
            tiles["x", g] = loaded.tile([P, 4096], BF16, name="x_or_w", bufs=2)
            nc.sync.dma_start(out=tiles["x", g][:, 0:2048], in_=x_hbm[:, g, :])

        def load_w(h, j_half):
            tiles["w", h, j_half] = loaded.tile([P, 4096], BF16, name="x_or_w", bufs=2)
            nc.sync.dma_start(
                out=tiles["w", h, j_half][:].rearrange("p (t w) -> p t w", t=4),
                in_=w_hbm[:, h, :, j_half * 1024 : (j_half + 1) * 1024],
            )

        x_w_loads = [
            lambda: load_w(0, 0),
            lambda: load_w(0, 1),
            lambda: load_x(0),
            lambda: load_x(1),
            lambda: load_w(1, 0),
            lambda: load_w(1, 1),
        ]

        def next_x_w_load():
            if len(x_w_loads) > 0:
                x_w_loads.pop(0)()

        def quantize_masked(codes, scales, k_pass):
            nc.vector.quantize_mx(
                out=codes[:, k_pass * 1024 : (k_pass + 1) * 1024].bitcast(E4M3),
                scales=scales[:, k_pass * 1024 : (k_pass + 1) * 1024],
                in_=masked[:].rearrange("p d j e t -> p (d j e t)"),
            )

        def sum_w_half(h):
            for j_half in range(2):
                for d in range(2):
                    later("w_sum", 4, lambda j_half=j_half, d=d: sum_w(h, j_half, d), 0 if j_half == 0 else 1)
            later("w_sum", 2, lambda: quantize_w(h))

        def sum_w(h, j_half, d):
            with nc.allow_low_precision(reason="the engine sums in float32 and rounds once to bfloat16"):
                nc.vector.tensor_reduce(
                    out=masked[:, d, j_half * 128 : (j_half + 1) * 128, d, :],
                    in_=tiles["w", h, j_half][:].rearrange("p (t j k d) -> p d j t k", t=4, j=128, k=4, d=2)[:, d],
                    axis=AXIS.X,
                    op=ALU.add,
                )
            if d == 1:
                next_x_w_load()

        def quantize_w(h):
            quantize_masked(w_codes, w_scales, h)
            if h == 0:
                interleave_x_later(0)
            else:
                there["w"] = 1

        def interleave_x_later(g):
            for d in (1, 0):
                later("copy", 2, lambda d=d: interleave_x(g, d), 1, True)

        def interleave_x(g, d):
            copy(
                out=masked[:, d, :, d, :],
                in_=tiles["x", g][:, 0:2048].rearrange("p (t j d) -> p d j t", t=4, j=256, d=2)[:, d],
            )
            if d == 1:
                next_x_w_load()
                later("vector", 2, lambda: quantize_x(g), 1, True)

        def quantize_x(g):
            quantize_masked(x_codes, x_scales, g)
            if g == 0:
                interleave_x_later(1)
            else:
                there["x"] = 1
                sum_w_half(1)

        def s_and_g(u):
            c, pair = u // 2, u % 2
            s_tdi = tiles["s", c][:, 2 * pair : 2 * pair + 2, :].rearrange("p t (i d) -> p t d i", d=2)
            g_tdi = tiles["g", c][:, 2 * pair : 2 * pair + 2, :].rearrange("p t (i d) -> p t d i", d=2)
            return s_tdi, g_tdi

        def new_narrow(what, u, bufs=2):
            tiles[what, u] = narrow.tile([P, 512], F32, name=what, bufs=bufs)
            return tiles[what, u]

        def square_s(u):
            tiles["s_sq", u] = wide.tile([P, 2, 2, 256], F32, name="s_sq", bufs=1)
            nc.scalar.activation(out=tiles["s_sq", u][:], in_=s_and_g(u)[0], func=ACT.Square)

        def multiply_g_s(u):
            s_tdi, g_tdi = s_and_g(u)
            tiles["g_s", u] = wide.tile([P, 2, 2, 256], F32, name="g_s")
            nc.gpsimd.tensor_tensor(out=tiles["g_s", u][:], in0=g_tdi, in1=s_tdi, op=ALU.mult)

        def add_over_d_transposed(src, dst):
            for t in range(2):
                for block in range(2):
                    col = (t * 2 + block) * 128
                    for d in range(2):
                        nc.tensor.matmul(
                            out=dst[:, col : col + 128],
                            lhsT=src[:, t, d, block * 128 : (block + 1) * 128],
                            rhs=identity[:],
                            is_transpose=True,
                            start=(d == 0),
                            stop=(d == 1),
                        )

        def make_n2_T(u):
            tiles["n2_T", u] = psum.tile([P, 512], F32, name="n2_T%d" % (u % 2))
            add_over_d_transposed(tiles["s_sq", u], tiles["n2_T", u])

        def make_p_T(u):
            tiles["p_T", u] = psum.tile([P, 512], F32, name="p_T_or_f")
            add_over_d_transposed(tiles["g_s", u], tiles["p_T", u])

        def make_rho(u):
            nc.scalar.activation(
                out=new_narrow("rho", u, 1)[:], in_=tiles["n2_T", u][:], func=ACT.Abs_reciprocal_sqrt, bias=tiny[:]
            )

        def make_n(u):
            nc.vector.tensor_tensor(
                out=new_narrow("n_then_f_T", u)[:], in0=tiles["n2_T", u][:], in1=tiles["rho", u][:], op=ALU.mult
            )

        def make_x(u):
            nc.gpsimd.tensor_scalar(
                out=new_narrow("x", u, 1)[:], in0=tiles["n_then_f_T", u][:], scalar1=1.0, scalar2=EPS, op0=ALU.mult, op1=ALU.add
            )

        def make_D(u):
            nc.vector.scalar_tensor_tensor(
                out=new_narrow("D_then_R", u)[:],
                in0=tiles["n2_T", u][:],
                scalar=1.0,
                in1=tiles["x", u][:],
                op0=ALU.add,
                op1=ALU.mult,
            )

        def make_n3_minus_n(u):
            nc.vector.scalar_tensor_tensor(
                out=new_narrow("n3_minus_n", u)[:],
                in0=tiles["n2_T", u][:],
                scalar=1.0,
                in1=tiles["n_then_f_T", u][:],
                op0=ALU.subtract,
                op1=ALU.mult,
            )

        def scalar_steps(u):
            d_then_r = tiles["D_then_R", u]
            nc.scalar.activation(out=d_then_r[:], in_=d_then_r[:], func=ACT.Abs_reciprocal_sqrt)
            nc.scalar.activation(out=d_then_r[:], in_=d_then_r[:], func=ACT.Square)
            nc.scalar.activation(out=new_narrow("R_squared", u)[:], in_=d_then_r[:], func=ACT.Square)

        def make_p_v(u):
            nc.vector.scalar_tensor_tensor(
                out=new_narrow("p_v_then_e_T", u)[:],
                in0=tiles["n3_minus_n", u][:],
                scalar=2.0 * EPS,
                in1=tiles["p_T", u][:],
                op0=ALU.subtract,
                op1=ALU.mult,
            )

        def make_f_T(u):
            nc.vector.tensor_tensor(
                out=tiles["n_then_f_T", u][:], in0=tiles["n2_T", u][:], in1=tiles["D_then_R", u][:], op=ALU.mult
            )

        def make_e_T(u):
            engine = nc.vector if u >= E_ON_VECTOR_FROM else nc.gpsimd
            engine.tensor_tensor(
                out=tiles["p_v_then_e_T", u][:], in0=tiles["p_v_then_e_T", u][:], in1=tiles["R_squared", u][:], op=ALU.mult
            )

        def transpose_back(src, dst):
            for col in range(0, 512, 128):
                nc.tensor.transpose(out=dst[:, col : col + 128], in_=src[:, col : col + 128], identity=identity[:])

        def bring_f_back(u):
            tiles["f", u] = psum.tile([P, 512], F32, name="p_T_or_f")
            transpose_back(tiles["n_then_f_T", u], tiles["f", u])

        def bring_e_back(u):
            tiles["e", u] = psum.tile([P, 512], F32, name="e")
            transpose_back(tiles["p_v_then_e_T", u], tiles["e", u])

        def for_both_d(bank):
            return bank[:].rearrange("p (t i) -> p t i", t=2).unsqueeze(2).to_broadcast([P, 2, 2, 256])

        def multiply_f_g(u):
            tiles["f_g", u] = wide.tile([P, 2, 2, 256], F32, name="f_g")
            nc.vector.tensor_tensor(out=tiles["f_g", u][:], in0=for_both_d(tiles["f", u]), in1=s_and_g(u)[1], op=ALU.mult)

        def multiply_e_s(u):
            tiles["e_s", u] = wide.tile([P, 2, 2, 256], F32, name="e_s")
            nc.vector.tensor_tensor(out=tiles["e_s", u][:], in0=for_both_d(tiles["e", u]), in1=s_and_g(u)[0], op=ALU.mult)

        def subtract(u):
            c, pair = u // 2, u % 2
            q, g = c // 2, c % 2
            h, second_quarter = q // 2, q % 2
            if second_quarter == 0 and pair == 0:
                tiles["ds", h, g] = staged.tile([P, 4, 2, 512], BF16, name="ds", align_bytes=64)
            engine = nc.vector if u >= SUBTRACT_ON_VECTOR_FROM else nc.gpsimd
            engine.tensor_tensor(
                out=tiles["ds", h, g][:, 2 * pair : 2 * pair + 2, :, second_quarter * 256 : (second_quarter + 1) * 256],
                in0=tiles["f_g", u][:],
                in1=tiles["e_s", u][:],
                op=ALU.subtract,
            )
            if second_quarter == 1:
                if pair == 0:
                    tiles["ds_T", c] = staged.tile([P, 4, 1024], BF16, name="ds_T", align_bytes=64)
                for t in (2 * pair, 2 * pair + 1):
                    later("tensor", 1, lambda t=t: turn(c, t), 0, False, ("turned",))
            if pair == 1:
                if g == 0:
                    tiles["ds_woven", q] = staged.tile([P, 2, 2, 256, 4], BF16, name="ds_woven", align_bytes=64)
                if c == LAST_CHUNK:
                    for d in (1, 0):
                        later("copy", 2, lambda d=d: weave(c, d), 0, True)
                else:
                    for d in (0, 1):
                        later("copy", 2, lambda d=d: weave(c, d), 0)

        def weave(c, d):
            q, g = c // 2, c % 2
            h, second_quarter = q // 2, q % 2
            copy(
                out=tiles["ds_woven", q][:, g, d].rearrange("p (c i) t -> p c t i", i=4),
                in_=tiles["ds", h, g][:, :, d, second_quarter * 256 : (second_quarter + 1) * 256].rearrange(
                    "p t (c i) -> p c t i", i=4
                ),
            )
            if d == 1 and (g == 1 or q >= 2):
                later("vector", 2, lambda: quantize_along_b(q, g), 1, c == LAST_CHUNK)

        def quantize_along_b(q, g):
            if g == 0 or q < 2:
                tiles["ds_codes", q] = staged.tile([P, 1024], U32, name="ds_codes", align_bytes=64)
                tiles["ds_scales", q] = staged.tile([P, 1024], U8, name="ds_scales", align_bytes=64)
            lo, hi = (0, 1024) if q < 2 else (g * 512, g * 512 + 512)
            nc.vector.quantize_mx(
                out=tiles["ds_codes", q][:, lo:hi].bitcast(E5M2),
                scales=tiles["ds_scales", q][:, lo:hi],
                in_=tiles["ds_woven", q][:].rearrange("p g d i t -> p (g d i t)")[:, 4 * lo : 4 * hi],
            )
            if g == 1:
                for block in (1, 0):
                    later("tensor", 2, lambda block=block: multiply_out_1(q, block), 0, True, ("x", "sum"))

        def multiply_out_1(q, block):
            bank, acc = take_bank("sum")
            for g in range(2):
                for d in range(2):
                    ds_col = g * 512 + d * 256 + block * 128
                    x_col = (g * 2 + d) * 512
                    nc.tensor.matmul_mx(
                        out=acc[:],
                        lhsT=tiles["ds_codes", q][:, ds_col : ds_col + 128].bitcast(E5M2),
                        lhsT_scale=tiles["ds_scales", q][:, ds_col : ds_col + 128],
                        rhs=x_codes[:, x_col : x_col + 512].bitcast(E4M3),
                        rhs_scale=x_scales[:, x_col : x_col + 512],
                        start=(g == 0 and d == 0),
                        stop=(g == 1 and d == 1),
                    )
            if q == 3:
                for j_half in (1, 0):
                    later("copy", 2, lambda j_half=j_half: store_out_1(q, block, j_half, acc, bank), 1, True)
            else:
                for j_half in (0, 1):
                    later("copy", 2, lambda j_half=j_half: store_out_1(q, block, j_half, acc, bank), 1)

        def store_out_1(q, block, j_half, acc, bank):
            repeated = staged.tile([P, 128, 4, 2], F32, name="repeated", bufs=3)
            copy(
                out=repeated[:],
                in_=acc[:, j_half * 256 : (j_half + 1) * 256]
                .rearrange("p (j d) -> p j d", d=2)
                .unsqueeze(2)
                .to_broadcast([P, 128, 4, 2]),
            )
            nc.sync.dma_start(
                out=out_1_hbm[:, q * 2 + block, j_half * 1024 : (j_half + 1) * 1024],
                in_=repeated[:].rearrange("p j k d -> p (j k d)"),
            )
            if j_half == 1:
                give_bank("sum", bank)

        def turn(c, t):
            q, g = c // 2, c % 2
            bank, turned = take_bank("turned")
            for d in range(2):
                words = tiles["ds", q // 2, g][:, t, d, :].bitcast(F32)
                for w in range(2):
                    col = (d * 2 + w) * 128
                    nc.tensor.transpose(out=turned[:, col : col + 128], in_=words[:, w:256:2], identity=identity[:])
            later("copy", 1, lambda: gather_turned(c, t, turned, bank), 1)

        def gather_turned(c, t, turned, bank):
            copy(
                out=tiles["ds_T", c][:, t].bitcast(F32).rearrange("p (d r w) -> p d r w", d=2, r=128, w=2),
                in_=turned[:].rearrange("p (d w r) -> p d r w", d=2, w=2, r=128),
            )
            give_bank("turned", bank)
            if t == 3 or (t == 1 and c >= LAST_CHUNK - 1):
                later("vector", 2, lambda: quantize_along_i(c, t), 1)

        def quantize_along_i(c, t_last):
            q, g = c // 2, c % 2
            h = q // 2
            t_first = 0 if c < LAST_CHUNK - 1 else t_last - 1
            lo, hi = g * 1024 + t_first * 256, g * 1024 + (t_last + 1) * 256
            nc.vector.quantize_mx(
                out=ds_T_codes[h][:, lo:hi].bitcast(E5M2),
                scales=ds_T_scales[h][:, lo:hi],
                in_=tiles["ds_T", c][:, t_first : t_last + 1].rearrange("p t w -> p (t w)"),
            )
            if h == 1:
                for t in range(t_first, t_last + 1):
                    later("tensor", 2, lambda t=t: multiply_out_0(g, t), 0, False, ("w", "sum"))

        def multiply_out_0(g, t):
            bank, acc = take_bank("sum")
            for h in range(2):
                for d in range(2):
                    ds_col = (g * 4 + t) * 256 + d * 128
                    w_col = (h * 2 + d) * 512
                    nc.tensor.matmul_mx(
                        out=acc[:],
                        lhsT=ds_T_codes[h][:, ds_col : ds_col + 128].bitcast(E5M2),
                        lhsT_scale=ds_T_scales[h][:, ds_col : ds_col + 128],
                        rhs=w_codes[:, w_col : w_col + 512].bitcast(E4M3),
                        rhs_scale=w_scales[:, w_col : w_col + 512],
                        start=(h == 0 and d == 0),
                        stop=(h == 1 and d == 1),
                    )
            later("copy", 1, lambda: store_out_0(g, t, acc, bank), 1)

        def store_out_0(g, t, acc, bank):
            rows = staged.tile([P, 512], F32, name="rows", bufs=3)
            copy(out=rows[:], in_=acc[:])
            give_bank("sum", bank)
            nc.sync.dma_start(out=out_0_hbm[:, g, t, :], in_=rows[:])

        def head():
            load_chunk(0, 0, 2)
            next_x_w_load()
            load_chunk(0, 2, 4)
            load_chunk(1, 0, 4)
            next_x_w_load()
            load_chunk(2, 0, 4)
            sum_w_half(0)
            square_s(0)
            make_n2_T(0)

        def one_round(r):
            def unit(u):
                return 0 <= u < UNITS

            this_round[0] = r
            if unit(r):
                make_rho(r)
            if unit(r - 2):
                multiply_f_g(r - 2)
            if unit(r - 3):
                subtract(r - 3)
                if r - 3 == UNITS - 1:
                    at_the_end[0] = True
                    for name in ("p_T_or_f", "e", "n2_T0", "n2_T1"):
                        give_bank("sum", name)
            if unit(r - 1):
                scalar_steps(r - 1)
            if unit(r):
                make_n(r)
            if unit(r - 1):
                make_p_T(r - 1)
            if unit(r):
                multiply_g_s(r)
            if unit(r - 2):
                multiply_e_s(r - 2)
                if r % 2 == 1 and (r - 3) // 2 + 3 <= LAST_CHUNK:
                    load_chunk((r - 3) // 2 + 3, 0, 4)
            if unit(r - 1):
                make_p_v(r - 1)
                make_f_T(r - 1)
            if unit(r + 1):
                square_s(r + 1)
            if unit(r - 1):
                bring_f_back(r - 1)
            if unit(r + 1):
                make_n2_T(r + 1)
            if unit(r):
                make_x(r)
            if r < SIDE_WORK_AT_THE_END_FROM:
                side_work()
            if unit(r):
                make_D(r)
                make_n3_minus_n(r)
            if unit(r - 1):
                make_e_T(r - 1)
                bring_e_back(r - 1)
            if r >= SIDE_WORK_AT_THE_END_FROM:
                side_work()

        with tc.manual_schedule():
            head()
            for r in range(PINNED):
                one_round(r)
        for r in range(PINNED, ROUNDS):
            one_round(r)
